import numpy as np
import ml_dtypes

BF16 = ml_dtypes.bfloat16


def bf(x):
    return np.asarray(x, np.float32).astype(BF16)


def f32(x):
    return np.asarray(x, np.float32)


def f64(x):
    return np.asarray(x).astype(np.float64)


def striped(idx):
    return np.tile(idx.reshape(-1, 16).T, (8, 1))


B, A, C, S, DEG, N, H, K, NB = 128, 3, 384, 512, 4, 2048, 256, 8, 8
BOX = 6.0
R_CUT = 2.5
SPAN = 0.45
ANG = BOX / (2.0 * np.pi)
SIGMA = R_CUT / NB


def setup_inputs():
    pos = f32(SPAN * BOX * np.random.random_sample((C, S)))
    idx = np.concatenate([np.random.permutation(S)[:H] for _ in range(K)])
    return {"pos": pos, "offs": striped(idx)}


def reference(pos, offs):
    idx = offs[:16].T.reshape(-1)
    p = f64(pos)
    ctr = np.repeat(p, DEG, axis=1)
    e = p[:, idx] + (-ctr)
    e = ANG * np.sin(e / ANG)
    e3 = e.reshape(A, B, N)
    r = (e3 ** 2).sum(axis=0)
    mu = np.linspace(0.0, R_CUT, NB)
    x = np.exp(-0.5 * ((r[:, :, None] - mu) / SIGMA) ** 2)
    xv = x[None] * e3[..., None]
    res = xv.reshape(A, B, S, DEG, NB).sum(axis=3)
    return res.reshape(C, S * NB)

@@ -1,0 +1,132 @@
+import math
+
+import concourse.mybir as mybir
+from concourse.masks import make_identity
+
+F32 = mybir.dt.float32
+BF16 = mybir.dt.bfloat16
+U16 = mybir.dt.uint16
+ACT = mybir.ActivationFunctionType
+ALU = mybir.AluOpType
+
+SAMPLES = 128
+COORDS = 3
+ATOMS = 512
+DEG = 4
+RADIAL = 8
+PIECE = 512
+PIECES = ATOMS * DEG // PIECE
+PIECE_ATOMS = PIECE // DEG
+BANK = 512
+BANK_ATOMS = BANK // RADIAL
+BANK_ENTRIES = BANK_ATOMS * DEG
+
+ANG = 6.0 / (2.0 * math.pi)
+SIGMA = 2.5 / RADIAL
+MIDDLE = 1.25
+NU = [2.5 * n / (RADIAL - 1) - MIDDLE for n in range(RADIAL)]
+COL_MIDDLE = RADIAL
+COL_LOG_ANG = RADIAL + 1
+
+
+def tile_graphembedlayer_kernel(tc, pos, offs, out):
+    nc = tc.nc
+    with (
+        tc.tile_pool(name="held", bufs=1) as held,
+        tc.tile_pool(name="ring", bufs=2) as ring,
+        tc.psum_pool(name="psum", bufs=6) as psum,
+    ):
+        offsets = held.tile([SAMPLES, ATOMS * DEG // 16], U16, name="offsets")
+        nc.sync.dma_start(offsets[:], offs)
+        table = [held.tile([SAMPLES, ATOMS], F32, name=f"table{a}") for a in range(COORDS)]
+        for a, queue in enumerate((nc.scalar, nc.gpsimd, nc.sync)):
+            queue.dma_start(table[a][:], pos[a * SAMPLES : (a + 1) * SAMPLES, :])
+
+        negated = [held.tile([SAMPLES, ATOMS * DEG], F32, name=f"negated{a}") for a in range(COORDS)]
+        for c in range(PIECES):
+            for a in range(COORDS):
+                nc.gpsimd.tensor_scalar_mul(
+                    negated[a][:, c * PIECE : (c + 1) * PIECE].rearrange("p (i t) -> p i t", t=DEG),
+                    table[a][:, c * PIECE_ATOMS : (c + 1) * PIECE_ATOMS]
+                    .unsqueeze(2)
+                    .to_broadcast([SAMPLES, PIECE_ATOMS, DEG]),
+                    -1.0,
+                )
+
+        biases = held.tile([SAMPLES, RADIAL + 2], F32, name="biases")
+        for n in range(RADIAL):
+            nc.gpsimd.memset(biases[:, n : n + 1], -(NU[n] * MIDDLE + NU[n] ** 2 / 2) / SIGMA**2)
+        nc.gpsimd.memset(biases[:, COL_MIDDLE : COL_MIDDLE + 1], -MIDDLE)
+        nc.gpsimd.memset(biases[:, COL_LOG_ANG : COL_LOG_ANG + 1], math.log(ANG))
+        identity = held.tile([SAMPLES, SAMPLES], BF16, name="identity")
+        make_identity(nc, identity[:])
+
+        sine = [held.tile([SAMPLES, ATOMS * DEG], F32, name=f"sine{a}") for a in range(COORDS)]
+        sum_sq = held.tile([SAMPLES, ATOMS * DEG], F32, name="sum_sq")
+        for c in range(PIECES):
+            entries = slice(c * PIECE, (c + 1) * PIECE)
+            squares = []
+            for a in range(COORDS):
+                diff = ring.tile([SAMPLES, PIECE], F32, name=f"diff{a}")
+                nc.vector.tensor_tensor(
+                    out=diff[:],
+                    in0=table[a][:].indirect(offsets[:, c * PIECE // 16 : (c + 1) * PIECE // 16]),
+                    in1=negated[a][:, entries],
+                    op=ALU.add,
+                )
+                nc.scalar.activation(out=sine[a][:, entries], in_=diff[:], func=ACT.Sin, scale=1.0 / ANG)
+                square = ring.tile([SAMPLES, PIECE], F32, name=f"square{a}")
+                nc.scalar.activation(out=square[:], in_=sine[a][:, entries], func=ACT.Square)
+                squares.append(square)
+            nc.gpsimd.tensor_add(sum_sq[:, entries], squares[0][:], squares[1][:])
+            nc.gpsimd.tensor_add(sum_sq[:, entries], sum_sq[:, entries], squares[2][:])
+
+        for c in range(PIECES):
+            entries = slice(c * PIECE, (c + 1) * PIECE)
+            rho_sq = ring.tile([SAMPLES, PIECE], F32, name="rho_sq")
+            nc.scalar.activation(
+                out=rho_sq[:], in_=sum_sq[:, entries], func=ACT.Square,
+                scale=ANG**2, bias=biases[:, COL_MIDDLE : COL_MIDDLE + 1],
+            )
+            envelope = ring.tile([SAMPLES, PIECE], F32, name="envelope")
+            nc.scalar.activation(
+                out=envelope[:], in_=rho_sq[:], func=ACT.Exp,
+                scale=-1.0 / (2.0 * SIGMA**2), bias=biases[:, COL_LOG_ANG : COL_LOG_ANG + 1],
+            )
+            weighted = ring.tile([SAMPLES, COORDS, PIECE], BF16, name="weighted")
+            for a in range(COORDS):
+                nc.gpsimd.tensor_mul(weighted[:, a, :], sine[a][:, entries], envelope[:])
+
+            radial = ring.tile([SAMPLES, RADIAL, PIECE], BF16, name="radial")
+            product = ring.tile([SAMPLES, COORDS, RADIAL, PIECE], BF16, name="product")
+            for n in range(RADIAL):
+                nc.scalar.activation(
+                    out=radial[:, n, :], in_=sum_sq[:, entries], func=ACT.Exp,
+                    scale=NU[n] * ANG**2 / SIGMA**2, bias=biases[:, n : n + 1],
+                )
+                nc.vector.tensor_tensor(
+                    out=product[:, :, n, :],
+                    in0=weighted[:],
+                    in1=radial[:, n, :].unsqueeze(1).to_broadcast([SAMPLES, COORDS, PIECE]),
+                    op=ALU.mult,
+                )
+
+            for a in range(COORDS):
+                staged = ring.tile([SAMPLES, PIECE_ATOMS * RADIAL], F32, name=f"staged{a}")
+                for h in range(PIECE // BANK_ENTRIES):
+                    by_neighbour = product[:, a, :, h * BANK_ENTRIES : (h + 1) * BANK_ENTRIES].rearrange(
+                        "p n (i t) -> p t i n", t=DEG
+                    )
+                    bank = psum.tile([SAMPLES, BANK], F32, name="bank")
+                    for t in range(DEG):
+                        nc.tensor.matmul(
+                            bank[:], identity[:], by_neighbour[:, t], start=(t == 0), stop=(t == DEG - 1)
+                        )
+                    if a < COORDS - 1:
+                        nc.scalar.copy(staged[:, h * BANK : (h + 1) * BANK], bank[:])
+                    else:
+                        nc.vector.tensor_copy(staged[:, h * BANK : (h + 1) * BANK], bank[:])
+                nc.sync.dma_start(
+                    out[a * SAMPLES : (a + 1) * SAMPLES, c * PIECE_ATOMS * RADIAL : (c + 1) * PIECE_ATOMS * RADIAL],
+                    staged[:],
+                )

@@ -19,13 +19,14 @@ PIECES = ATOMS * DEG // PIECE
 PIECE_ATOMS = PIECE // DEG
 BANK = 512
 BANK_ATOMS = BANK // RADIAL
-BANK_ENTRIES = BANK_ATOMS * DEG
 
 ANG = 6.0 / (2.0 * math.pi)
 SIGMA = 2.5 / RADIAL
-MIDDLE = 1.25
-NU = [2.5 * n / (RADIAL - 1) - MIDDLE for n in range(RADIAL)]
-COL_MIDDLE = RADIAL
+MU = [2.5 * n / (RADIAL - 1) for n in range(RADIAL)]
+PIVOT = 4
+NU = [MU[n] - MU[PIVOT] for n in range(RADIAL)]
+OTHERS = [n for n in range(RADIAL) if n != PIVOT]
+COL_PIVOT = RADIAL
 COL_LOG_ANG = RADIAL + 1
 
 
@@ -33,100 +34,104 @@ def tile_graphembedlayer_kernel(tc, pos, offs, out):
     nc = tc.nc
     with (
         tc.tile_pool(name="held", bufs=1) as held,
-        tc.tile_pool(name="ring", bufs=2) as ring,
-        tc.psum_pool(name="psum", bufs=6) as psum,
+        tc.tile_pool(name="ring", bufs=3) as ring,
+        tc.psum_pool(name="psum_q", bufs=PIECES) as psum_q,
+        tc.psum_pool(name="psum_out", bufs=4) as psum_out,
     ):
         offsets = held.tile([SAMPLES, ATOMS * DEG // 16], U16, name="offsets")
         nc.sync.dma_start(offsets[:], offs)
         table = [held.tile([SAMPLES, ATOMS], F32, name=f"table{a}") for a in range(COORDS)]
-        for a, queue in enumerate((nc.scalar, nc.gpsimd, nc.sync)):
+        for a, queue in enumerate((nc.scalar, nc.sync, nc.scalar)):
             queue.dma_start(table[a][:], pos[a * SAMPLES : (a + 1) * SAMPLES, :])
 
-        negated = [held.tile([SAMPLES, ATOMS * DEG], F32, name=f"negated{a}") for a in range(COORDS)]
+        biases = held.tile([SAMPLES, RADIAL + 2], F32, name="biases")
+        for n in OTHERS:
+            nc.gpsimd.memset(biases[:, n : n + 1], -(NU[n] * MU[PIVOT] + NU[n] ** 2 / 2) / SIGMA**2)
+        nc.gpsimd.memset(biases[:, COL_PIVOT : COL_PIVOT + 1], -MU[PIVOT])
+        nc.gpsimd.memset(biases[:, COL_LOG_ANG : COL_LOG_ANG + 1], math.log(ANG))
+        identity_f32 = held.tile([SAMPLES, SAMPLES], F32, name="identity_f32")
+        make_identity(nc, identity_f32[:])
+        identity_bf16 = held.tile([SAMPLES, SAMPLES], BF16, name="identity_bf16")
+        make_identity(nc, identity_bf16[:])
+
+        sine = [held.tile([SAMPLES, COORDS, PIECE], F32, name=f"sine{c}") for c in range(PIECES)]
+        sum_sq = []
         for c in range(PIECES):
+            q = psum_q.tile([SAMPLES, PIECE], F32, name="q")
+            sum_sq.append(q)
             for a in range(COORDS):
-                nc.gpsimd.tensor_scalar_mul(
-                    negated[a][:, c * PIECE : (c + 1) * PIECE].rearrange("p (i t) -> p i t", t=DEG),
+                negated = ring.tile([SAMPLES, PIECE_ATOMS, DEG], F32, name="negated")
+                nc.vector.tensor_scalar_mul(
+                    negated[:],
                     table[a][:, c * PIECE_ATOMS : (c + 1) * PIECE_ATOMS]
                     .unsqueeze(2)
                     .to_broadcast([SAMPLES, PIECE_ATOMS, DEG]),
                     -1.0,
                 )
-
-        biases = held.tile([SAMPLES, RADIAL + 2], F32, name="biases")
-        for n in range(RADIAL):
-            nc.gpsimd.memset(biases[:, n : n + 1], -(NU[n] * MIDDLE + NU[n] ** 2 / 2) / SIGMA**2)
-        nc.gpsimd.memset(biases[:, COL_MIDDLE : COL_MIDDLE + 1], -MIDDLE)
-        nc.gpsimd.memset(biases[:, COL_LOG_ANG : COL_LOG_ANG + 1], math.log(ANG))
-        identity = held.tile([SAMPLES, SAMPLES], BF16, name="identity")
-        make_identity(nc, identity[:])
-
-        sine = [held.tile([SAMPLES, ATOMS * DEG], F32, name=f"sine{a}") for a in range(COORDS)]
-        sum_sq = held.tile([SAMPLES, ATOMS * DEG], F32, name="sum_sq")
-        for c in range(PIECES):
-            entries = slice(c * PIECE, (c + 1) * PIECE)
-            squares = []
-            for a in range(COORDS):
-                diff = ring.tile([SAMPLES, PIECE], F32, name=f"diff{a}")
+                diff = ring.tile([SAMPLES, PIECE], F32, name="diff")
                 nc.vector.tensor_tensor(
                     out=diff[:],
                     in0=table[a][:].indirect(offsets[:, c * PIECE // 16 : (c + 1) * PIECE // 16]),
-                    in1=negated[a][:, entries],
+                    in1=negated[:].rearrange("p i t -> p (i t)"),
                     op=ALU.add,
                 )
-                nc.scalar.activation(out=sine[a][:, entries], in_=diff[:], func=ACT.Sin, scale=1.0 / ANG)
-                square = ring.tile([SAMPLES, PIECE], F32, name=f"square{a}")
-                nc.scalar.activation(out=square[:], in_=sine[a][:, entries], func=ACT.Square)
-                squares.append(square)
-            nc.gpsimd.tensor_add(sum_sq[:, entries], squares[0][:], squares[1][:])
-            nc.gpsimd.tensor_add(sum_sq[:, entries], sum_sq[:, entries], squares[2][:])
+                nc.scalar.activation(
+                    out=sine[c][:, a, :].rearrange("p (t i) -> p t i", t=DEG),
+                    in_=diff[:].rearrange("p (i t) -> p t i", t=DEG),
+                    func=ACT.Sin,
+                    scale=1.0 / ANG,
+                )
+                square = ring.tile([SAMPLES, PIECE], F32, name="square")
+                nc.scalar.activation(out=square[:], in_=sine[c][:, a, :], func=ACT.Square)
+                nc.tensor.matmul(q[:], identity_f32[:], square[:], start=(a == 0), stop=(a == COORDS - 1))
 
         for c in range(PIECES):
-            entries = slice(c * PIECE, (c + 1) * PIECE)
+            q = sum_sq[c]
+            product = ring.tile([SAMPLES, COORDS, RADIAL, PIECE], BF16, name="product")
             rho_sq = ring.tile([SAMPLES, PIECE], F32, name="rho_sq")
             nc.scalar.activation(
-                out=rho_sq[:], in_=sum_sq[:, entries], func=ACT.Square,
-                scale=ANG**2, bias=biases[:, COL_MIDDLE : COL_MIDDLE + 1],
+                out=rho_sq[:], in_=q[:], func=ACT.Square,
+                scale=ANG**2, bias=biases[:, COL_PIVOT : COL_PIVOT + 1],
             )
             envelope = ring.tile([SAMPLES, PIECE], F32, name="envelope")
             nc.scalar.activation(
                 out=envelope[:], in_=rho_sq[:], func=ACT.Exp,
                 scale=-1.0 / (2.0 * SIGMA**2), bias=biases[:, COL_LOG_ANG : COL_LOG_ANG + 1],
             )
-            weighted = ring.tile([SAMPLES, COORDS, PIECE], BF16, name="weighted")
-            for a in range(COORDS):
-                nc.gpsimd.tensor_mul(weighted[:, a, :], sine[a][:, entries], envelope[:])
-
-            radial = ring.tile([SAMPLES, RADIAL, PIECE], BF16, name="radial")
-            product = ring.tile([SAMPLES, COORDS, RADIAL, PIECE], BF16, name="product")
-            for n in range(RADIAL):
+            weighted = product[:, :, PIVOT, :]
+            nc.vector.tensor_tensor(
+                out=weighted,
+                in0=sine[c][:],
+                in1=envelope[:].unsqueeze(1).to_broadcast([SAMPLES, COORDS, PIECE]),
+                op=ALU.mult,
+            )
+            for n in OTHERS:
+                radial = ring.tile([SAMPLES, PIECE], BF16, name="radial")
                 nc.scalar.activation(
-                    out=radial[:, n, :], in_=sum_sq[:, entries], func=ACT.Exp,
+                    out=radial[:], in_=q[:], func=ACT.Exp,
                     scale=NU[n] * ANG**2 / SIGMA**2, bias=biases[:, n : n + 1],
                 )
                 nc.vector.tensor_tensor(
                     out=product[:, :, n, :],
-                    in0=weighted[:],
-                    in1=radial[:, n, :].unsqueeze(1).to_broadcast([SAMPLES, COORDS, PIECE]),
+                    in0=weighted,
+                    in1=radial[:].unsqueeze(1).to_broadcast([SAMPLES, COORDS, PIECE]),
                     op=ALU.mult,
                 )
 
             for a in range(COORDS):
-                staged = ring.tile([SAMPLES, PIECE_ATOMS * RADIAL], F32, name=f"staged{a}")
-                for h in range(PIECE // BANK_ENTRIES):
-                    by_neighbour = product[:, a, :, h * BANK_ENTRIES : (h + 1) * BANK_ENTRIES].rearrange(
-                        "p n (i t) -> p t i n", t=DEG
-                    )
-                    bank = psum.tile([SAMPLES, BANK], F32, name="bank")
+                staged = ring.tile([SAMPLES, PIECE_ATOMS, RADIAL], F32, name="staged")
+                for h in range(PIECE_ATOMS // BANK_ATOMS):
+                    bank = psum_out.tile([SAMPLES, RADIAL, BANK_ATOMS], F32, name="bank")
                     for t in range(DEG):
+                        first = t * PIECE_ATOMS + h * BANK_ATOMS
                         nc.tensor.matmul(
-                            bank[:], identity[:], by_neighbour[:, t], start=(t == 0), stop=(t == DEG - 1)
+                            bank[:], identity_bf16[:], product[:, a, :, first : first + BANK_ATOMS],
+                            start=(t == 0), stop=(t == DEG - 1),
                         )
-                    if a < COORDS - 1:
-                        nc.scalar.copy(staged[:, h * BANK : (h + 1) * BANK], bank[:])
-                    else:
-                        nc.vector.tensor_copy(staged[:, h * BANK : (h + 1) * BANK], bank[:])
+                    nc.scalar.copy(
+                        staged[:, h * BANK_ATOMS : (h + 1) * BANK_ATOMS, :], bank[:].rearrange("p n i -> p i n")
+                    )
                 nc.sync.dma_start(
                     out[a * SAMPLES : (a + 1) * SAMPLES, c * PIECE_ATOMS * RADIAL : (c + 1) * PIECE_ATOMS * RADIAL],
-                    staged[:],
+                    staged[:].rearrange("p i n -> p (i n)"),
                 )

@@ -35,6 +35,7 @@ def tile_graphembedlayer_kernel(tc, pos, offs, out):
     with (
         tc.tile_pool(name="held", bufs=1) as held,
         tc.tile_pool(name="ring", bufs=3) as ring,
+        tc.tile_pool(name="stage", bufs=6) as stage,
         tc.psum_pool(name="psum_q", bufs=PIECES) as psum_q,
         tc.psum_pool(name="psum_out", bufs=4) as psum_out,
     ):
@@ -56,6 +57,14 @@ def tile_graphembedlayer_kernel(tc, pos, offs, out):
 
         sine = [held.tile([SAMPLES, COORDS, PIECE], F32, name=f"sine{c}") for c in range(PIECES)]
         sum_sq = []
+        rho_sq = [held.tile([SAMPLES, PIECE], F32, name=f"rho_sq{c}") for c in range(PIECES)]
+
+        def square_rho(c):
+            nc.scalar.activation(
+                out=rho_sq[c][:], in_=sum_sq[c][:], func=ACT.Square,
+                scale=ANG**2, bias=biases[:, COL_PIVOT : COL_PIVOT + 1],
+            )
+
         for c in range(PIECES):
             q = psum_q.tile([SAMPLES, PIECE], F32, name="q")
             sum_sq.append(q)
@@ -84,42 +93,45 @@ def tile_graphembedlayer_kernel(tc, pos, offs, out):
                 square = ring.tile([SAMPLES, PIECE], F32, name="square")
                 nc.scalar.activation(out=square[:], in_=sine[c][:, a, :], func=ACT.Square)
                 nc.tensor.matmul(q[:], identity_f32[:], square[:], start=(a == 0), stop=(a == COORDS - 1))
+            if c > 0:
+                square_rho(c - 1)
+
+        sine_bf16 = [held.tile([SAMPLES, COORDS, PIECE], BF16, name=f"sine_bf16_{c}") for c in range(PIECES)]
+        for c in range(PIECES):
+            nc.vector.tensor_copy(sine_bf16[c][:], sine[c][:])
 
         for c in range(PIECES):
             q = sum_sq[c]
             product = ring.tile([SAMPLES, COORDS, RADIAL, PIECE], BF16, name="product")
-            rho_sq = ring.tile([SAMPLES, PIECE], F32, name="rho_sq")
+            if c == PIECES - 1:
+                square_rho(c)
+            envelope = ring.tile([SAMPLES, PIECE], BF16, name="envelope")
             nc.scalar.activation(
-                out=rho_sq[:], in_=q[:], func=ACT.Square,
-                scale=ANG**2, bias=biases[:, COL_PIVOT : COL_PIVOT + 1],
-            )
-            envelope = ring.tile([SAMPLES, PIECE], F32, name="envelope")
-            nc.scalar.activation(
-                out=envelope[:], in_=rho_sq[:], func=ACT.Exp,
+                out=envelope[:], in_=rho_sq[c][:], func=ACT.Exp,
                 scale=-1.0 / (2.0 * SIGMA**2), bias=biases[:, COL_LOG_ANG : COL_LOG_ANG + 1],
             )
             weighted = product[:, :, PIVOT, :]
             nc.vector.tensor_tensor(
                 out=weighted,
-                in0=sine[c][:],
+                in0=sine_bf16[c][:],
                 in1=envelope[:].unsqueeze(1).to_broadcast([SAMPLES, COORDS, PIECE]),
                 op=ALU.mult,
             )
+            radial = ring.tile([SAMPLES, RADIAL, PIECE], BF16, name="radial")
             for n in OTHERS:
-                radial = ring.tile([SAMPLES, PIECE], BF16, name="radial")
                 nc.scalar.activation(
-                    out=radial[:], in_=q[:], func=ACT.Exp,
+                    out=radial[:, n, :], in_=q[:], func=ACT.Exp,
                     scale=NU[n] * ANG**2 / SIGMA**2, bias=biases[:, n : n + 1],
-                )
-                nc.vector.tensor_tensor(
-                    out=product[:, :, n, :],
-                    in0=weighted,
-                    in1=radial[:].unsqueeze(1).to_broadcast([SAMPLES, COORDS, PIECE]),
-                    op=ALU.mult,
                 )
 
             for a in range(COORDS):
-                staged = ring.tile([SAMPLES, PIECE_ATOMS, RADIAL], F32, name="staged")
+                for low, high in ((0, PIVOT), (PIVOT + 1, RADIAL)):
+                    nc.vector.tensor_tensor(
+                        out=product[:, a, low:high, :],
+                        in0=radial[:, low:high, :],
+                        in1=product[:, a, PIVOT : PIVOT + 1, :].to_broadcast([SAMPLES, high - low, PIECE]),
+                        op=ALU.mult,
+                    )
                 for h in range(PIECE_ATOMS // BANK_ATOMS):
                     bank = psum_out.tile([SAMPLES, RADIAL, BANK_ATOMS], F32, name="bank")
                     for t in range(DEG):
@@ -128,10 +140,10 @@ def tile_graphembedlayer_kernel(tc, pos, offs, out):
                             bank[:], identity_bf16[:], product[:, a, :, first : first + BANK_ATOMS],
                             start=(t == 0), stop=(t == DEG - 1),
                         )
-                    nc.scalar.copy(
-                        staged[:, h * BANK_ATOMS : (h + 1) * BANK_ATOMS, :], bank[:].rearrange("p n i -> p i n")
+                    staged = stage.tile([SAMPLES, BANK_ATOMS, RADIAL], F32, name="staged")
+                    nc.any.tensor_copy(staged[:], bank[:].rearrange("p n i -> p i n"))
+                    column = (c * PIECE_ATOMS + h * BANK_ATOMS) * RADIAL
+                    nc.sync.dma_start(
+                        out[a * SAMPLES : (a + 1) * SAMPLES, column : column + BANK],
+                        staged[:].rearrange("p i n -> p (i n)"),
                     )
-                nc.sync.dma_start(
-                    out[a * SAMPLES : (a + 1) * SAMPLES, c * PIECE_ATOMS * RADIAL : (c + 1) * PIECE_ATOMS * RADIAL],
-                    staged[:].rearrange("p i n -> p (i n)"),
-                )

@@ -84,12 +84,7 @@ def tile_graphembedlayer_kernel(tc, pos, offs, out):
                     in1=negated[:].rearrange("p i t -> p (i t)"),
                     op=ALU.add,
                 )
-                nc.scalar.activation(
-                    out=sine[c][:, a, :].rearrange("p (t i) -> p t i", t=DEG),
-                    in_=diff[:].rearrange("p (i t) -> p t i", t=DEG),
-                    func=ACT.Sin,
-                    scale=1.0 / ANG,
-                )
+                nc.scalar.activation(out=sine[c][:, a, :], in_=diff[:], func=ACT.Sin, scale=1.0 / ANG)
                 square = ring.tile([SAMPLES, PIECE], F32, name="square")
                 nc.scalar.activation(out=square[:], in_=sine[c][:, a, :], func=ACT.Square)
                 nc.tensor.matmul(q[:], identity_f32[:], square[:], start=(a == 0), stop=(a == COORDS - 1))
@@ -132,12 +127,12 @@ def tile_graphembedlayer_kernel(tc, pos, offs, out):
                         in1=product[:, a, PIVOT : PIVOT + 1, :].to_broadcast([SAMPLES, high - low, PIECE]),
                         op=ALU.mult,
                     )
+                by_neighbour = product[:, a, :, :].rearrange("p n (i t) -> p t n i", t=DEG)
                 for h in range(PIECE_ATOMS // BANK_ATOMS):
                     bank = psum_out.tile([SAMPLES, RADIAL, BANK_ATOMS], F32, name="bank")
                     for t in range(DEG):
-                        first = t * PIECE_ATOMS + h * BANK_ATOMS
                         nc.tensor.matmul(
-                            bank[:], identity_bf16[:], product[:, a, :, first : first + BANK_ATOMS],
+                            bank[:], identity_bf16[:], by_neighbour[:, t, :, h * BANK_ATOMS : (h + 1) * BANK_ATOMS],
                             start=(t == 0), stop=(t == DEG - 1),
                         )
                     staged = stage.tile([SAMPLES, BANK_ATOMS, RADIAL], F32, name="staged")

@@ -18,16 +18,17 @@ PIECE = 512
 PIECES = ATOMS * DEG // PIECE
 PIECE_ATOMS = PIECE // DEG
 BANK = 512
-BANK_ATOMS = BANK // RADIAL
+BLOCK_ATOMS = BANK // RADIAL
+BLOCK = BLOCK_ATOMS * DEG
+PIECE_BLOCKS = PIECE // BLOCK
 
 ANG = 6.0 / (2.0 * math.pi)
 SIGMA = 2.5 / RADIAL
 MU = [2.5 * n / (RADIAL - 1) for n in range(RADIAL)]
-PIVOT = 4
+PIVOT = RADIAL - 1
 NU = [MU[n] - MU[PIVOT] for n in range(RADIAL)]
-OTHERS = [n for n in range(RADIAL) if n != PIVOT]
-COL_PIVOT = RADIAL
-COL_LOG_ANG = RADIAL + 1
+COL_PIVOT = PIVOT
+COL_LOG_ANG = PIVOT + 1
 
 
 def tile_graphembedlayer_kernel(tc, pos, offs, out):
@@ -45,8 +46,8 @@ def tile_graphembedlayer_kernel(tc, pos, offs, out):
         for a, queue in enumerate((nc.scalar, nc.sync, nc.scalar)):
             queue.dma_start(table[a][:], pos[a * SAMPLES : (a + 1) * SAMPLES, :])
 
-        biases = held.tile([SAMPLES, RADIAL + 2], F32, name="biases")
-        for n in OTHERS:
+        biases = held.tile([SAMPLES, PIVOT + 2], F32, name="biases")
+        for n in range(PIVOT):
             nc.gpsimd.memset(biases[:, n : n + 1], -(NU[n] * MU[PIVOT] + NU[n] ** 2 / 2) / SIGMA**2)
         nc.gpsimd.memset(biases[:, COL_PIVOT : COL_PIVOT + 1], -MU[PIVOT])
         nc.gpsimd.memset(biases[:, COL_LOG_ANG : COL_LOG_ANG + 1], math.log(ANG))
@@ -84,7 +85,12 @@ def tile_graphembedlayer_kernel(tc, pos, offs, out):
                     in1=negated[:].rearrange("p i t -> p (i t)"),
                     op=ALU.add,
                 )
-                nc.scalar.activation(out=sine[c][:, a, :], in_=diff[:], func=ACT.Sin, scale=1.0 / ANG)
+                nc.scalar.activation(
+                    out=sine[c][:, a, :].rearrange("p (h t i) -> p h i t", t=DEG, i=BLOCK_ATOMS),
+                    in_=diff[:].rearrange("p (h i t) -> p h i t", t=DEG, i=BLOCK_ATOMS),
+                    func=ACT.Sin,
+                    scale=1.0 / ANG,
+                )
                 square = ring.tile([SAMPLES, PIECE], F32, name="square")
                 nc.scalar.activation(out=square[:], in_=sine[c][:, a, :], func=ACT.Square)
                 nc.tensor.matmul(q[:], identity_f32[:], square[:], start=(a == 0), stop=(a == COORDS - 1))
@@ -95,49 +101,44 @@ def tile_graphembedlayer_kernel(tc, pos, offs, out):
         for c in range(PIECES):
             nc.vector.tensor_copy(sine_bf16[c][:], sine[c][:])
 
+        square_rho(PIECES - 1)
         for c in range(PIECES):
-            q = sum_sq[c]
-            product = ring.tile([SAMPLES, COORDS, RADIAL, PIECE], BF16, name="product")
-            if c == PIECES - 1:
-                square_rho(c)
-            envelope = ring.tile([SAMPLES, PIECE], BF16, name="envelope")
-            nc.scalar.activation(
-                out=envelope[:], in_=rho_sq[c][:], func=ACT.Exp,
-                scale=-1.0 / (2.0 * SIGMA**2), bias=biases[:, COL_LOG_ANG : COL_LOG_ANG + 1],
-            )
-            weighted = product[:, :, PIVOT, :]
-            nc.vector.tensor_tensor(
-                out=weighted,
-                in0=sine_bf16[c][:],
-                in1=envelope[:].unsqueeze(1).to_broadcast([SAMPLES, COORDS, PIECE]),
-                op=ALU.mult,
-            )
-            radial = ring.tile([SAMPLES, RADIAL, PIECE], BF16, name="radial")
-            for n in OTHERS:
+            for h in range(PIECE_BLOCKS):
+                entries = slice(h * BLOCK, (h + 1) * BLOCK)
+                envelope = ring.tile([SAMPLES, BLOCK], BF16, name="envelope")
                 nc.scalar.activation(
-                    out=radial[:, n, :], in_=q[:], func=ACT.Exp,
-                    scale=NU[n] * ANG**2 / SIGMA**2, bias=biases[:, n : n + 1],
+                    out=envelope[:], in_=rho_sq[c][:, entries], func=ACT.Exp,
+                    scale=-1.0 / (2.0 * SIGMA**2), bias=biases[:, COL_LOG_ANG : COL_LOG_ANG + 1],
                 )
-
-            for a in range(COORDS):
-                for low, high in ((0, PIVOT), (PIVOT + 1, RADIAL)):
+                product = ring.tile([SAMPLES, COORDS, RADIAL, BLOCK], BF16, name="product")
+                nc.vector.tensor_tensor(
+                    out=product[:, :, PIVOT, :],
+                    in0=sine_bf16[c][:, :, entries],
+                    in1=envelope[:].unsqueeze(1).to_broadcast([SAMPLES, COORDS, BLOCK]),
+                    op=ALU.mult,
+                )
+                radial = ring.tile([SAMPLES, PIVOT, BLOCK], BF16, name="radial")
+                for n in range(PIVOT):
+                    nc.scalar.activation(
+                        out=radial[:, n, :], in_=sum_sq[c][:, entries], func=ACT.Exp,
+                        scale=NU[n] * ANG**2 / SIGMA**2, bias=biases[:, n : n + 1],
+                    )
+                for a in range(COORDS):
                     nc.vector.tensor_tensor(
-                        out=product[:, a, low:high, :],
-                        in0=radial[:, low:high, :],
-                        in1=product[:, a, PIVOT : PIVOT + 1, :].to_broadcast([SAMPLES, high - low, PIECE]),
+                        out=product[:, a, 0:PIVOT, :],
+                        in0=radial[:],
+                        in1=product[:, a, PIVOT : PIVOT + 1, :].to_broadcast([SAMPLES, PIVOT, BLOCK]),
                         op=ALU.mult,
                     )
-                by_neighbour = product[:, a, :, :].rearrange("p n (i t) -> p t n i", t=DEG)
-                for h in range(PIECE_ATOMS // BANK_ATOMS):
-                    bank = psum_out.tile([SAMPLES, RADIAL, BANK_ATOMS], F32, name="bank")
+                    bank = psum_out.tile([SAMPLES, RADIAL, BLOCK_ATOMS], F32, name="bank")
                     for t in range(DEG):
                         nc.tensor.matmul(
-                            bank[:], identity_bf16[:], by_neighbour[:, t, :, h * BANK_ATOMS : (h + 1) * BANK_ATOMS],
+                            bank[:], identity_bf16[:], product[:, a, :, t * BLOCK_ATOMS : (t + 1) * BLOCK_ATOMS],
                             start=(t == 0), stop=(t == DEG - 1),
                         )
-                    staged = stage.tile([SAMPLES, BANK_ATOMS, RADIAL], F32, name="staged")
+                    staged = stage.tile([SAMPLES, BLOCK_ATOMS, RADIAL], F32, name="staged")
                     nc.any.tensor_copy(staged[:], bank[:].rearrange("p n i -> p i n"))
-                    column = (c * PIECE_ATOMS + h * BANK_ATOMS) * RADIAL
+                    column = (c * PIECE_BLOCKS + h) * BANK
                     nc.sync.dma_start(
                         out[a * SAMPLES : (a + 1) * SAMPLES, column : column + BANK],
                         staged[:].rearrange("p i n -> p (i n)"),

@@ -66,23 +66,23 @@ def tile_graphembedlayer_kernel(tc, pos, offs, out):
                 scale=ANG**2, bias=biases[:, COL_PIVOT : COL_PIVOT + 1],
             )
 
+        negated = [held.tile([SAMPLES, ATOMS * DEG], F32, name=f"negated{a}") for a in range(COORDS)]
+        for a in range(COORDS):
+            nc.vector.tensor_scalar_mul(
+                negated[a][:].rearrange("p (i t) -> p i t", t=DEG),
+                table[a][:].unsqueeze(2).to_broadcast([SAMPLES, ATOMS, DEG]),
+                -1.0,
+            )
+
         for c in range(PIECES):
             q = psum_q.tile([SAMPLES, PIECE], F32, name="q")
             sum_sq.append(q)
             for a in range(COORDS):
-                negated = ring.tile([SAMPLES, PIECE_ATOMS, DEG], F32, name="negated")
-                nc.vector.tensor_scalar_mul(
-                    negated[:],
-                    table[a][:, c * PIECE_ATOMS : (c + 1) * PIECE_ATOMS]
-                    .unsqueeze(2)
-                    .to_broadcast([SAMPLES, PIECE_ATOMS, DEG]),
-                    -1.0,
-                )
                 diff = ring.tile([SAMPLES, PIECE], F32, name="diff")
                 nc.vector.tensor_tensor(
                     out=diff[:],
                     in0=table[a][:].indirect(offsets[:, c * PIECE // 16 : (c + 1) * PIECE // 16]),
-                    in1=negated[:].rearrange("p i t -> p (i t)"),
+                    in1=negated[a][:, c * PIECE : (c + 1) * PIECE],
                     op=ALU.add,
                 )
                 nc.scalar.activation(
@@ -101,8 +101,9 @@ def tile_graphembedlayer_kernel(tc, pos, offs, out):
         for c in range(PIECES):
             nc.vector.tensor_copy(sine_bf16[c][:], sine[c][:])
 
-        square_rho(PIECES - 1)
         for c in range(PIECES):
+            if c == PIECES - 1:
+                square_rho(c)
             for h in range(PIECE_BLOCKS):
                 entries = slice(h * BLOCK, (h + 1) * BLOCK)
                 envelope = ring.tile([SAMPLES, BLOCK], BF16, name="envelope")

@@ -68,11 +68,11 @@ def tile_graphembedlayer_kernel(tc, pos, offs, out):
 
         negated = [held.tile([SAMPLES, ATOMS * DEG], F32, name=f"negated{a}") for a in range(COORDS)]
         for a in range(COORDS):
-            nc.vector.tensor_scalar_mul(
-                negated[a][:].rearrange("p (i t) -> p i t", t=DEG),
-                table[a][:].unsqueeze(2).to_broadcast([SAMPLES, ATOMS, DEG]),
-                -1.0,
-            )
+            repeated = table[a][:].unsqueeze(2).to_broadcast([SAMPLES, ATOMS, DEG])
+            if a == 1:
+                nc.scalar.mul(negated[a][:].rearrange("p (i t) -> p i t", t=DEG), repeated, -1.0)
+            else:
+                nc.vector.tensor_scalar_mul(negated[a][:].rearrange("p (i t) -> p i t", t=DEG), repeated, -1.0)
 
         for c in range(PIECES):
             q = psum_q.tile([SAMPLES, PIECE], F32, name="q")
@@ -91,11 +91,21 @@ def tile_graphembedlayer_kernel(tc, pos, offs, out):
                     func=ACT.Sin,
                     scale=1.0 / ANG,
                 )
-                square = ring.tile([SAMPLES, PIECE], F32, name="square")
-                nc.scalar.activation(out=square[:], in_=sine[c][:, a, :], func=ACT.Square)
-                nc.tensor.matmul(q[:], identity_f32[:], square[:], start=(a == 0), stop=(a == COORDS - 1))
+                if c < PIECES - 1:
+                    square = ring.tile([SAMPLES, PIECE], F32, name="square")
+                    nc.scalar.activation(out=square[:], in_=sine[c][:, a, :], func=ACT.Square)
+                    nc.tensor.matmul(q[:], identity_f32[:], square[:], start=(a == 0), stop=(a == COORDS - 1))
             if c > 0:
                 square_rho(c - 1)
+
+        for a in range(COORDS):
+            square = ring.tile([SAMPLES, PIECE], F32, name="square")
+            nc.vector.tensor_tensor(
+                out=square[:], in0=sine[PIECES - 1][:, a, :], in1=sine[PIECES - 1][:, a, :], op=ALU.mult
+            )
+            nc.tensor.matmul(
+                sum_sq[PIECES - 1][:], identity_f32[:], square[:], start=(a == 0), stop=(a == COORDS - 1)
+            )
 
         sine_bf16 = [held.tile([SAMPLES, COORDS, PIECE], BF16, name=f"sine_bf16_{c}") for c in range(PIECES)]
         for c in range(PIECES):

@@ -16,8 +16,8 @@ DEG = 4
 RADIAL = 8
 PIECE = 512
 PIECES = ATOMS * DEG // PIECE
-PIECE_ATOMS = PIECE // DEG
 BANK = 512
+BANKS = 8
 BLOCK_ATOMS = BANK // RADIAL
 BLOCK = BLOCK_ATOMS * DEG
 PIECE_BLOCKS = PIECE // BLOCK
@@ -37,8 +37,7 @@ def tile_graphembedlayer_kernel(tc, pos, offs, out):
         tc.tile_pool(name="held", bufs=1) as held,
         tc.tile_pool(name="ring", bufs=3) as ring,
         tc.tile_pool(name="stage", bufs=6) as stage,
-        tc.psum_pool(name="psum_q", bufs=PIECES) as psum_q,
-        tc.psum_pool(name="psum_out", bufs=4) as psum_out,
+        tc.psum_pool(name="psum", bufs=BANKS) as psum,
     ):
         offsets = held.tile([SAMPLES, ATOMS * DEG // 16], U16, name="offsets")
         nc.sync.dma_start(offsets[:], offs)
@@ -56,13 +55,13 @@ def tile_graphembedlayer_kernel(tc, pos, offs, out):
         identity_bf16 = held.tile([SAMPLES, SAMPLES], BF16, name="identity_bf16")
         make_identity(nc, identity_bf16[:])
 
-        sine = [held.tile([SAMPLES, COORDS, PIECE], F32, name=f"sine{c}") for c in range(PIECES)]
-        sum_sq = []
-        rho_sq = [held.tile([SAMPLES, PIECE], F32, name=f"rho_sq{c}") for c in range(PIECES)]
+        sine = [held.tile([SAMPLES, COORDS, PIECE], F32, name=f"sine{k}") for k in range(PIECES)]
+        q = []
+        rho_sq = [held.tile([SAMPLES, PIECE], F32, name=f"rho_sq{k}") for k in range(PIECES)]
 
-        def square_rho(c):
+        def square_rho(k):
             nc.scalar.activation(
-                out=rho_sq[c][:], in_=sum_sq[c][:], func=ACT.Square,
+                out=rho_sq[k][:], in_=q[k][:], func=ACT.Square,
                 scale=ANG**2, bias=biases[:, COL_PIVOT : COL_PIVOT + 1],
             )
 
@@ -74,29 +73,28 @@ def tile_graphembedlayer_kernel(tc, pos, offs, out):
             else:
                 nc.vector.tensor_scalar_mul(negated[a][:].rearrange("p (i t) -> p i t", t=DEG), repeated, -1.0)
 
-        for c in range(PIECES):
-            q = psum_q.tile([SAMPLES, PIECE], F32, name="q")
-            sum_sq.append(q)
+        for k in range(PIECES):
+            q.append(psum.tile([SAMPLES, PIECE], F32, name="q", tag="bank"))
             for a in range(COORDS):
                 diff = ring.tile([SAMPLES, PIECE], F32, name="diff")
                 nc.vector.tensor_tensor(
                     out=diff[:],
-                    in0=table[a][:].indirect(offsets[:, c * PIECE // 16 : (c + 1) * PIECE // 16]),
-                    in1=negated[a][:, c * PIECE : (c + 1) * PIECE],
+                    in0=table[a][:].indirect(offsets[:, k * PIECE // 16 : (k + 1) * PIECE // 16]),
+                    in1=negated[a][:, k * PIECE : (k + 1) * PIECE],
                     op=ALU.add,
                 )
                 nc.scalar.activation(
-                    out=sine[c][:, a, :].rearrange("p (h t i) -> p h i t", t=DEG, i=BLOCK_ATOMS),
+                    out=sine[k][:, a, :].rearrange("p (h t i) -> p h i t", t=DEG, i=BLOCK_ATOMS),
                     in_=diff[:].rearrange("p (h i t) -> p h i t", t=DEG, i=BLOCK_ATOMS),
                     func=ACT.Sin,
                     scale=1.0 / ANG,
                 )
-                if c < PIECES - 1:
+                if k < PIECES - 1:
                     square = ring.tile([SAMPLES, PIECE], F32, name="square")
-                    nc.scalar.activation(out=square[:], in_=sine[c][:, a, :], func=ACT.Square)
-                    nc.tensor.matmul(q[:], identity_f32[:], square[:], start=(a == 0), stop=(a == COORDS - 1))
-            if c > 0:
-                square_rho(c - 1)
+                    nc.scalar.activation(out=square[:], in_=sine[k][:, a, :], func=ACT.Square)
+                    nc.tensor.matmul(q[k][:], identity_f32[:], square[:], start=(a == 0), stop=(a == COORDS - 1))
+            if k > 0:
+                square_rho(k - 1)
 
         for a in range(COORDS):
             square = ring.tile([SAMPLES, PIECE], F32, name="square")
@@ -104,34 +102,34 @@ def tile_graphembedlayer_kernel(tc, pos, offs, out):
                 out=square[:], in0=sine[PIECES - 1][:, a, :], in1=sine[PIECES - 1][:, a, :], op=ALU.mult
             )
             nc.tensor.matmul(
-                sum_sq[PIECES - 1][:], identity_f32[:], square[:], start=(a == 0), stop=(a == COORDS - 1)
+                q[PIECES - 1][:], identity_f32[:], square[:], start=(a == 0), stop=(a == COORDS - 1)
             )
 
-        sine_bf16 = [held.tile([SAMPLES, COORDS, PIECE], BF16, name=f"sine_bf16_{c}") for c in range(PIECES)]
-        for c in range(PIECES):
-            nc.vector.tensor_copy(sine_bf16[c][:], sine[c][:])
+        sine_bf16 = [held.tile([SAMPLES, COORDS, PIECE], BF16, name=f"sine_bf16_{k}") for k in range(PIECES)]
+        for k in range(PIECES):
+            nc.vector.tensor_copy(sine_bf16[k][:], sine[k][:])
 
-        for c in range(PIECES):
-            if c == PIECES - 1:
-                square_rho(c)
+        for k in range(PIECES):
+            if k == PIECES - 1:
+                square_rho(k)
             for h in range(PIECE_BLOCKS):
                 entries = slice(h * BLOCK, (h + 1) * BLOCK)
                 envelope = ring.tile([SAMPLES, BLOCK], BF16, name="envelope")
                 nc.scalar.activation(
-                    out=envelope[:], in_=rho_sq[c][:, entries], func=ACT.Exp,
+                    out=envelope[:], in_=rho_sq[k][:, entries], func=ACT.Exp,
                     scale=-1.0 / (2.0 * SIGMA**2), bias=biases[:, COL_LOG_ANG : COL_LOG_ANG + 1],
                 )
                 product = ring.tile([SAMPLES, COORDS, RADIAL, BLOCK], BF16, name="product")
                 nc.vector.tensor_tensor(
                     out=product[:, :, PIVOT, :],
-                    in0=sine_bf16[c][:, :, entries],
+                    in0=sine_bf16[k][:, :, entries],
                     in1=envelope[:].unsqueeze(1).to_broadcast([SAMPLES, COORDS, BLOCK]),
                     op=ALU.mult,
                 )
                 radial = ring.tile([SAMPLES, PIVOT, BLOCK], BF16, name="radial")
                 for n in range(PIVOT):
                     nc.scalar.activation(
-                        out=radial[:, n, :], in_=sum_sq[c][:, entries], func=ACT.Exp,
+                        out=radial[:, n, :], in_=q[k][:, entries], func=ACT.Exp,
                         scale=NU[n] * ANG**2 / SIGMA**2, bias=biases[:, n : n + 1],
                     )
                 for a in range(COORDS):
@@ -141,7 +139,7 @@ def tile_graphembedlayer_kernel(tc, pos, offs, out):
                         in1=product[:, a, PIVOT : PIVOT + 1, :].to_broadcast([SAMPLES, PIVOT, BLOCK]),
                         op=ALU.mult,
                     )
-                    bank = psum_out.tile([SAMPLES, RADIAL, BLOCK_ATOMS], F32, name="bank")
+                    bank = psum.tile([SAMPLES, RADIAL, BLOCK_ATOMS], F32, name="bank", tag="bank")
                     for t in range(DEG):
                         nc.tensor.matmul(
                             bank[:], identity_bf16[:], product[:, a, :, t * BLOCK_ATOMS : (t + 1) * BLOCK_ATOMS],
@@ -149,7 +147,7 @@ def tile_graphembedlayer_kernel(tc, pos, offs, out):
                         )
                     staged = stage.tile([SAMPLES, BLOCK_ATOMS, RADIAL], F32, name="staged")
                     nc.any.tensor_copy(staged[:], bank[:].rearrange("p n i -> p i n"))
-                    column = (c * PIECE_BLOCKS + h) * BANK
+                    column = (k * PIECE_BLOCKS + h) * BANK
                     nc.sync.dma_start(
                         out[a * SAMPLES : (a + 1) * SAMPLES, column : column + BANK],
                         staged[:].rearrange("p i n -> p (i n)"),

@@ -21,14 +21,19 @@ BANKS = 8
 BLOCK_ATOMS = BANK // RADIAL
 BLOCK = BLOCK_ATOMS * DEG
 PIECE_BLOCKS = PIECE // BLOCK
+BLOCKS = PIECES * PIECE_BLOCKS
+AHEAD = 2
 
 ANG = 6.0 / (2.0 * math.pi)
 SIGMA = 2.5 / RADIAL
 MU = [2.5 * n / (RADIAL - 1) for n in range(RADIAL)]
 PIVOT = RADIAL - 1
-NU = [MU[n] - MU[PIVOT] for n in range(RADIAL)]
-COL_PIVOT = PIVOT
-COL_LOG_ANG = PIVOT + 1
+DELTA = MU[1] - MU[0]
+FACTORS = ((1, 0), (2, 1), (2, 0), (4, 0))
+FULL = 3
+LACK = [math.exp(-4.0 * (FULL - n) * DELTA**2 / SIGMA**2) for n in range(FULL)]
+COL_PIVOT = len(FACTORS)
+COL_LOG_ANG = len(FACTORS) + 1
 
 
 def tile_graphembedlayer_kernel(tc, pos, offs, out):
@@ -36,6 +41,7 @@ def tile_graphembedlayer_kernel(tc, pos, offs, out):
     with (
         tc.tile_pool(name="held", bufs=1) as held,
         tc.tile_pool(name="ring", bufs=3) as ring,
+        tc.tile_pool(name="ahead", bufs=AHEAD + 2) as ahead,
         tc.tile_pool(name="stage", bufs=6) as stage,
         tc.psum_pool(name="psum", bufs=BANKS) as psum,
     ):
@@ -45,17 +51,22 @@ def tile_graphembedlayer_kernel(tc, pos, offs, out):
         for a, queue in enumerate((nc.scalar, nc.sync, nc.scalar)):
             queue.dma_start(table[a][:], pos[a * SAMPLES : (a + 1) * SAMPLES, :])
 
-        biases = held.tile([SAMPLES, PIVOT + 2], F32, name="biases")
-        for n in range(PIVOT):
-            nc.gpsimd.memset(biases[:, n : n + 1], -(NU[n] * MU[PIVOT] + NU[n] ** 2 / 2) / SIGMA**2)
+        biases = held.tile([SAMPLES, len(FACTORS) + 2], F32, name="biases")
+        for f, (m, d) in enumerate(FACTORS):
+            nc.gpsimd.memset(
+                biases[:, f : f + 1], (m * DELTA * MU[PIVOT] - ((d + m) ** 2 - d**2) * DELTA**2 / 2) / SIGMA**2
+            )
         nc.gpsimd.memset(biases[:, COL_PIVOT : COL_PIVOT + 1], -MU[PIVOT])
         nc.gpsimd.memset(biases[:, COL_LOG_ANG : COL_LOG_ANG + 1], math.log(ANG))
         identity_f32 = held.tile([SAMPLES, SAMPLES], F32, name="identity_f32")
         make_identity(nc, identity_f32[:])
         identity_bf16 = held.tile([SAMPLES, SAMPLES], BF16, name="identity_bf16")
         make_identity(nc, identity_bf16[:])
+        lacking = held.tile([SAMPLES, FULL, SAMPLES], BF16, name="lacking")
+        for n in range(FULL):
+            nc.scalar.mul(lacking[:, n, :], identity_f32[:], LACK[n])
 
-        sine = [held.tile([SAMPLES, COORDS, PIECE], F32, name=f"sine{k}") for k in range(PIECES)]
+        sine = [held.tile([SAMPLES, COORDS, PIECE], BF16, name=f"sine{k}") for k in range(PIECES)]
         q = []
         rho_sq = [held.tile([SAMPLES, PIECE], F32, name=f"rho_sq{k}") for k in range(PIECES)]
 
@@ -105,50 +116,75 @@ def tile_graphembedlayer_kernel(tc, pos, offs, out):
                 q[PIECES - 1][:], identity_f32[:], square[:], start=(a == 0), stop=(a == COORDS - 1)
             )
 
-        sine_bf16 = [held.tile([SAMPLES, COORDS, PIECE], BF16, name=f"sine_bf16_{k}") for k in range(PIECES)]
-        for k in range(PIECES):
-            nc.vector.tensor_copy(sine_bf16[k][:], sine[k][:])
+        envelope, factors, product = {}, {}, {}
 
-        for k in range(PIECES):
-            if k == PIECES - 1:
+        def exponentials(u):
+            k, h = divmod(u, PIECE_BLOCKS)
+            entries = slice(h * BLOCK, (h + 1) * BLOCK)
+            if k == PIECES - 1 and h == 0:
                 square_rho(k)
-            for h in range(PIECE_BLOCKS):
-                entries = slice(h * BLOCK, (h + 1) * BLOCK)
-                envelope = ring.tile([SAMPLES, BLOCK], BF16, name="envelope")
+            envelope[u] = ahead.tile([SAMPLES, BLOCK], BF16, name="envelope")
+            nc.scalar.activation(
+                out=envelope[u][:], in_=rho_sq[k][:, entries], func=ACT.Exp,
+                scale=-1.0 / (2.0 * SIGMA**2), bias=biases[:, COL_LOG_ANG : COL_LOG_ANG + 1],
+            )
+            factors[u] = ahead.tile([SAMPLES, len(FACTORS), BLOCK], BF16, name="factors")
+            for f, (m, d) in enumerate(FACTORS):
                 nc.scalar.activation(
-                    out=envelope[:], in_=rho_sq[k][:, entries], func=ACT.Exp,
-                    scale=-1.0 / (2.0 * SIGMA**2), bias=biases[:, COL_LOG_ANG : COL_LOG_ANG + 1],
+                    out=factors[u][:, f, :], in_=q[k][:, entries], func=ACT.Exp,
+                    scale=-m * DELTA * ANG**2 / SIGMA**2, bias=biases[:, f : f + 1],
                 )
-                product = ring.tile([SAMPLES, COORDS, RADIAL, BLOCK], BF16, name="product")
-                nc.vector.tensor_tensor(
-                    out=product[:, :, PIVOT, :],
-                    in0=sine_bf16[k][:, :, entries],
-                    in1=envelope[:].unsqueeze(1).to_broadcast([SAMPLES, COORDS, BLOCK]),
-                    op=ALU.mult,
-                )
-                radial = ring.tile([SAMPLES, PIVOT, BLOCK], BF16, name="radial")
-                for n in range(PIVOT):
-                    nc.scalar.activation(
-                        out=radial[:, n, :], in_=q[k][:, entries], func=ACT.Exp,
-                        scale=NU[n] * ANG**2 / SIGMA**2, bias=biases[:, n : n + 1],
+
+        def pivot_products(u):
+            k, h = divmod(u, PIECE_BLOCKS)
+            product[u] = ring.tile([SAMPLES, COORDS, RADIAL, BLOCK], BF16, name="product")
+            nc.vector.tensor_tensor(
+                out=product[u][:, :, PIVOT, :],
+                in0=sine[k][:, :, h * BLOCK : (h + 1) * BLOCK],
+                in1=envelope[u][:].unsqueeze(1).to_broadcast([SAMPLES, COORDS, BLOCK]),
+                op=ALU.mult,
+            )
+
+        def double(u, m, rows, coords):
+            low = RADIAL - 2 * m
+            nc.vector.tensor_tensor(
+                out=product[u][:, coords, low : low + m, :],
+                in0=product[u][:, coords, low + m : low + 2 * m, :],
+                in1=factors[u][:, rows, :].unsqueeze(1).to_broadcast([SAMPLES, coords.stop - coords.start, m, BLOCK]),
+                op=ALU.mult,
+            )
+
+        def sum_neighbours(u, a):
+            bank = psum.tile([SAMPLES, RADIAL, BLOCK_ATOMS], F32, name="bank", tag="bank")
+            for functions, weight in [(slice(FULL, RADIAL), identity_bf16[:])] + [
+                (slice(n, n + 1), lacking[:, n, :]) for n in range(FULL)
+            ]:
+                for t in range(DEG):
+                    nc.tensor.matmul(
+                        bank[:, functions, :], weight,
+                        product[u][:, a, functions, t * BLOCK_ATOMS : (t + 1) * BLOCK_ATOMS],
+                        start=(t == 0), stop=(t == DEG - 1),
                     )
-                for a in range(COORDS):
-                    nc.vector.tensor_tensor(
-                        out=product[:, a, 0:PIVOT, :],
-                        in0=radial[:],
-                        in1=product[:, a, PIVOT : PIVOT + 1, :].to_broadcast([SAMPLES, PIVOT, BLOCK]),
-                        op=ALU.mult,
-                    )
-                    bank = psum.tile([SAMPLES, RADIAL, BLOCK_ATOMS], F32, name="bank", tag="bank")
-                    for t in range(DEG):
-                        nc.tensor.matmul(
-                            bank[:], identity_bf16[:], product[:, a, :, t * BLOCK_ATOMS : (t + 1) * BLOCK_ATOMS],
-                            start=(t == 0), stop=(t == DEG - 1),
-                        )
-                    staged = stage.tile([SAMPLES, BLOCK_ATOMS, RADIAL], F32, name="staged")
-                    nc.any.tensor_copy(staged[:], bank[:].rearrange("p n i -> p i n"))
-                    column = (k * PIECE_BLOCKS + h) * BANK
-                    nc.sync.dma_start(
-                        out[a * SAMPLES : (a + 1) * SAMPLES, column : column + BANK],
-                        staged[:].rearrange("p i n -> p (i n)"),
-                    )
+            staged = stage.tile([SAMPLES, BLOCK_ATOMS, RADIAL], F32, name="staged")
+            nc.any.tensor_copy(staged[:], bank[:].rearrange("p n i -> p i n"))
+            nc.sync.dma_start(
+                out[a * SAMPLES : (a + 1) * SAMPLES, u * BANK : (u + 1) * BANK],
+                staged[:].rearrange("p i n -> p (i n)"),
+            )
+
+        for u in range(AHEAD):
+            exponentials(u)
+        for u in range(BLOCKS + 1):
+            if u + AHEAD < BLOCKS:
+                exponentials(u + AHEAD)
+            for a in range(COORDS):
+                if u < BLOCKS:
+                    if a == 0:
+                        pivot_products(u)
+                    elif a == 1:
+                        double(u, 1, slice(0, 1), slice(0, COORDS))
+                    else:
+                        double(u, 2, slice(1, 3), slice(0, COORDS))
+                if u > 0:
+                    double(u - 1, 4, slice(3, 4), slice(a, a + 1))
+                    sum_neighbours(u - 1, a)

@@ -42,6 +42,7 @@ def tile_graphembedlayer_kernel(tc, pos, offs, out):
         tc.tile_pool(name="held", bufs=1) as held,
         tc.tile_pool(name="ring", bufs=3) as ring,
         tc.tile_pool(name="ahead", bufs=AHEAD + 2) as ahead,
+        tc.tile_pool(name="lag", bufs=6) as lag,
         tc.tile_pool(name="stage", bufs=6) as stage,
         tc.psum_pool(name="psum", bufs=BANKS) as psum,
     ):
@@ -58,6 +59,8 @@ def tile_graphembedlayer_kernel(tc, pos, offs, out):
             )
         nc.gpsimd.memset(biases[:, COL_PIVOT : COL_PIVOT + 1], -MU[PIVOT])
         nc.gpsimd.memset(biases[:, COL_LOG_ANG : COL_LOG_ANG + 1], math.log(ANG))
+        warm = held.tile([SAMPLES, 1], F32, name="warm")
+        nc.scalar.activation(out=warm[:], in_=biases[:, 0:1], func=ACT.Sin, scale=0.0)
         identity_f32 = held.tile([SAMPLES, SAMPLES], F32, name="identity_f32")
         make_identity(nc, identity_f32[:])
         identity_bf16 = held.tile([SAMPLES, SAMPLES], BF16, name="identity_bf16")
@@ -87,7 +90,7 @@ def tile_graphembedlayer_kernel(tc, pos, offs, out):
         for k in range(PIECES):
             q.append(psum.tile([SAMPLES, PIECE], F32, name="q", tag="bank"))
             for a in range(COORDS):
-                diff = ring.tile([SAMPLES, PIECE], F32, name="diff")
+                diff = lag.tile([SAMPLES, PIECE], F32, name="diff")
                 nc.vector.tensor_tensor(
                     out=diff[:],
                     in0=table[a][:].indirect(offsets[:, k * PIECE // 16 : (k + 1) * PIECE // 16]),
@@ -104,8 +107,8 @@ def tile_graphembedlayer_kernel(tc, pos, offs, out):
                     square = ring.tile([SAMPLES, PIECE], F32, name="square")
                     nc.scalar.activation(out=square[:], in_=sine[k][:, a, :], func=ACT.Square)
                     nc.tensor.matmul(q[k][:], identity_f32[:], square[:], start=(a == 0), stop=(a == COORDS - 1))
-            if k > 0:
-                square_rho(k - 1)
+            if k == 1:
+                square_rho(0)
 
         for a in range(COORDS):
             square = ring.tile([SAMPLES, PIECE], F32, name="square")
@@ -121,7 +124,7 @@ def tile_graphembedlayer_kernel(tc, pos, offs, out):
         def exponentials(u):
             k, h = divmod(u, PIECE_BLOCKS)
             entries = slice(h * BLOCK, (h + 1) * BLOCK)
-            if k == PIECES - 1 and h == 0:
+            if k > 0 and h == 0:
                 square_rho(k)
             envelope[u] = ahead.tile([SAMPLES, BLOCK], BF16, name="envelope")
             nc.scalar.activation(

@@ -49,7 +49,7 @@ def tile_graphembedlayer_kernel(tc, pos, offs, out):
         offsets = held.tile([SAMPLES, ATOMS * DEG // 16], U16, name="offsets")
         nc.sync.dma_start(offsets[:], offs)
         table = [held.tile([SAMPLES, ATOMS], F32, name=f"table{a}") for a in range(COORDS)]
-        for a, queue in enumerate((nc.scalar, nc.sync, nc.scalar)):
+        for a, queue in ((0, nc.scalar), (2, nc.sync), (1, nc.sync)):
             queue.dma_start(table[a][:], pos[a * SAMPLES : (a + 1) * SAMPLES, :])
 
         biases = held.tile([SAMPLES, len(FACTORS) + 2], F32, name="biases")
@@ -80,16 +80,21 @@ def tile_graphembedlayer_kernel(tc, pos, offs, out):
             )
 
         negated = [held.tile([SAMPLES, ATOMS * DEG], F32, name=f"negated{a}") for a in range(COORDS)]
-        for a in range(COORDS):
-            repeated = table[a][:].unsqueeze(2).to_broadcast([SAMPLES, ATOMS, DEG])
-            if a == 1:
-                nc.scalar.mul(negated[a][:].rearrange("p (i t) -> p i t", t=DEG), repeated, -1.0)
-            else:
-                nc.vector.tensor_scalar_mul(negated[a][:].rearrange("p (i t) -> p i t", t=DEG), repeated, -1.0)
+
+        def negate(a, multiply):
+            multiply(
+                negated[a][:].rearrange("p (i t) -> p i t", t=DEG),
+                table[a][:].unsqueeze(2).to_broadcast([SAMPLES, ATOMS, DEG]),
+                -1.0,
+            )
+
+        negate(COORDS - 1, nc.scalar.mul)
 
         for k in range(PIECES):
             q.append(psum.tile([SAMPLES, PIECE], F32, name="q", tag="bank"))
             for a in range(COORDS):
+                if k == 0 and a < COORDS - 1:
+                    negate(a, nc.vector.tensor_scalar_mul)
                 diff = lag.tile([SAMPLES, PIECE], F32, name="diff")
                 nc.vector.tensor_tensor(
                     out=diff[:],
@@ -157,17 +162,21 @@ def tile_graphembedlayer_kernel(tc, pos, offs, out):
                 op=ALU.mult,
             )
 
-        def sum_neighbours(u, a):
+        def sum_neighbours(bank, u, a, functions, weight):
+            for t in range(DEG):
+                nc.tensor.matmul(
+                    bank[:, functions, :], weight,
+                    product[u][:, a, functions, t * BLOCK_ATOMS : (t + 1) * BLOCK_ATOMS],
+                    start=(t == 0), stop=(t == DEG - 1),
+                )
+
+        def finish(u, a):
             bank = psum.tile([SAMPLES, RADIAL, BLOCK_ATOMS], F32, name="bank", tag="bank")
-            for functions, weight in [(slice(FULL, RADIAL), identity_bf16[:])] + [
-                (slice(n, n + 1), lacking[:, n, :]) for n in range(FULL)
-            ]:
-                for t in range(DEG):
-                    nc.tensor.matmul(
-                        bank[:, functions, :], weight,
-                        product[u][:, a, functions, t * BLOCK_ATOMS : (t + 1) * BLOCK_ATOMS],
-                        start=(t == 0), stop=(t == DEG - 1),
-                    )
+            sum_neighbours(bank, u, a, slice(RADIAL // 2, RADIAL), identity_bf16[:])
+            double(u, 4, slice(3, 4), slice(a, a + 1))
+            sum_neighbours(bank, u, a, slice(FULL, RADIAL // 2), identity_bf16[:])
+            for n in range(FULL):
+                sum_neighbours(bank, u, a, slice(n, n + 1), lacking[:, n, :])
             staged = stage.tile([SAMPLES, BLOCK_ATOMS, RADIAL], F32, name="staged")
             nc.any.tensor_copy(staged[:], bank[:].rearrange("p n i -> p i n"))
             nc.sync.dma_start(
@@ -189,5 +198,4 @@ def tile_graphembedlayer_kernel(tc, pos, offs, out):
                     else:
                         double(u, 2, slice(1, 3), slice(0, COORDS))
                 if u > 0:
-                    double(u - 1, 4, slice(3, 4), slice(a, a + 1))
-                    sum_neighbours(u - 1, a)
+                    finish(u - 1, a)

@@ -14,6 +14,7 @@ COORDS = 3
 ATOMS = 512
 DEG = 4
 RADIAL = 8
+HALF = RADIAL // 2
 PIECE = 512
 PIECES = ATOMS * DEG // PIECE
 BANK = 512
@@ -43,6 +44,7 @@ def tile_graphembedlayer_kernel(tc, pos, offs, out):
         tc.tile_pool(name="ring", bufs=3) as ring,
         tc.tile_pool(name="ahead", bufs=AHEAD + 2) as ahead,
         tc.tile_pool(name="lag", bufs=6) as lag,
+        tc.tile_pool(name="lows", bufs=6) as lows,
         tc.tile_pool(name="stage", bufs=6) as stage,
         tc.psum_pool(name="psum", bufs=BANKS) as psum,
     ):
@@ -124,7 +126,7 @@ def tile_graphembedlayer_kernel(tc, pos, offs, out):
                 q[PIECES - 1][:], identity_f32[:], square[:], start=(a == 0), stop=(a == COORDS - 1)
             )
 
-        envelope, factors, product = {}, {}, {}
+        envelope, factors, upper, bank = {}, {}, {}, {}
 
         def exponentials(u):
             k, h = divmod(u, PIECE_BLOCKS)
@@ -145,40 +147,47 @@ def tile_graphembedlayer_kernel(tc, pos, offs, out):
 
         def pivot_products(u):
             k, h = divmod(u, PIECE_BLOCKS)
-            product[u] = ring.tile([SAMPLES, COORDS, RADIAL, BLOCK], BF16, name="product")
+            upper[u] = ring.tile([SAMPLES, COORDS, HALF, BLOCK], BF16, name="upper")
             nc.vector.tensor_tensor(
-                out=product[u][:, :, PIVOT, :],
+                out=upper[u][:, :, PIVOT - HALF, :],
                 in0=sine[k][:, :, h * BLOCK : (h + 1) * BLOCK],
                 in1=envelope[u][:].unsqueeze(1).to_broadcast([SAMPLES, COORDS, BLOCK]),
                 op=ALU.mult,
             )
 
-        def double(u, m, rows, coords):
-            low = RADIAL - 2 * m
+        def double(u, m, rows):
+            low = HALF - 2 * m
             nc.vector.tensor_tensor(
-                out=product[u][:, coords, low : low + m, :],
-                in0=product[u][:, coords, low + m : low + 2 * m, :],
-                in1=factors[u][:, rows, :].unsqueeze(1).to_broadcast([SAMPLES, coords.stop - coords.start, m, BLOCK]),
+                out=upper[u][:, :, low : low + m, :],
+                in0=upper[u][:, :, low + m : low + 2 * m, :],
+                in1=factors[u][:, rows, :].unsqueeze(1).to_broadcast([SAMPLES, COORDS, m, BLOCK]),
                 op=ALU.mult,
             )
 
-        def sum_neighbours(bank, u, a, functions, weight):
+        def sum_neighbours(columns, weight, products):
             for t in range(DEG):
                 nc.tensor.matmul(
-                    bank[:, functions, :], weight,
-                    product[u][:, a, functions, t * BLOCK_ATOMS : (t + 1) * BLOCK_ATOMS],
+                    columns, weight, products[:, :, t * BLOCK_ATOMS : (t + 1) * BLOCK_ATOMS],
                     start=(t == 0), stop=(t == DEG - 1),
                 )
 
+        def begin(u, a):
+            bank[u, a] = psum.tile([SAMPLES, RADIAL, BLOCK_ATOMS], F32, name="bank", tag="bank")
+            sum_neighbours(bank[u, a][:, HALF:RADIAL, :], identity_bf16[:], upper[u][:, a, :, :])
+
         def finish(u, a):
-            bank = psum.tile([SAMPLES, RADIAL, BLOCK_ATOMS], F32, name="bank", tag="bank")
-            sum_neighbours(bank, u, a, slice(RADIAL // 2, RADIAL), identity_bf16[:])
-            double(u, 4, slice(3, 4), slice(a, a + 1))
-            sum_neighbours(bank, u, a, slice(FULL, RADIAL // 2), identity_bf16[:])
+            lower = lows.tile([SAMPLES, HALF, BLOCK], BF16, name="lower")
+            nc.vector.tensor_tensor(
+                out=lower[:],
+                in0=upper[u][:, a, :, :],
+                in1=factors[u][:, 3:4, :].to_broadcast([SAMPLES, HALF, BLOCK]),
+                op=ALU.mult,
+            )
+            sum_neighbours(bank[u, a][:, FULL:HALF, :], identity_bf16[:], lower[:, FULL:HALF, :])
             for n in range(FULL):
-                sum_neighbours(bank, u, a, slice(n, n + 1), lacking[:, n, :])
+                sum_neighbours(bank[u, a][:, n : n + 1, :], lacking[:, n, :], lower[:, n : n + 1, :])
             staged = stage.tile([SAMPLES, BLOCK_ATOMS, RADIAL], F32, name="staged")
-            nc.any.tensor_copy(staged[:], bank[:].rearrange("p n i -> p i n"))
+            nc.any.tensor_copy(staged[:], bank[u, a][:].rearrange("p n i -> p i n"))
             nc.sync.dma_start(
                 out[a * SAMPLES : (a + 1) * SAMPLES, u * BANK : (u + 1) * BANK],
                 staged[:].rearrange("p i n -> p (i n)"),
@@ -194,8 +203,10 @@ def tile_graphembedlayer_kernel(tc, pos, offs, out):
                     if a == 0:
                         pivot_products(u)
                     elif a == 1:
-                        double(u, 1, slice(0, 1), slice(0, COORDS))
+                        double(u, 1, slice(0, 1))
                     else:
-                        double(u, 2, slice(1, 3), slice(0, COORDS))
+                        double(u, 2, slice(1, 3))
+                        for c in range(COORDS):
+                            begin(u, c)
                 if u > 0:
                     finish(u - 1, a)

@@ -49,10 +49,12 @@ def tile_graphembedlayer_kernel(tc, pos, offs, out):
         tc.psum_pool(name="psum", bufs=BANKS) as psum,
     ):
         offsets = held.tile([SAMPLES, ATOMS * DEG // 16], U16, name="offsets")
-        nc.sync.dma_start(offsets[:], offs)
         table = [held.tile([SAMPLES, ATOMS], F32, name=f"table{a}") for a in range(COORDS)]
-        for a, queue in ((0, nc.scalar), (2, nc.sync), (1, nc.sync)):
-            queue.dma_start(table[a][:], pos[a * SAMPLES : (a + 1) * SAMPLES, :])
+        nc.sync.dma_start(table[0][0 : SAMPLES // 2, :], pos[0 : SAMPLES // 2, :])
+        nc.scalar.dma_start(table[0][SAMPLES // 2 : SAMPLES, :], pos[SAMPLES // 2 : SAMPLES, :])
+        nc.sync.dma_start(offsets[:], offs)
+        nc.sync.dma_start(table[2][:], pos[2 * SAMPLES : 3 * SAMPLES, :])
+        nc.scalar.dma_start(table[1][:], pos[SAMPLES : 2 * SAMPLES, :])
 
         biases = held.tile([SAMPLES, len(FACTORS) + 2], F32, name="biases")
         for f, (m, d) in enumerate(FACTORS):
@@ -155,12 +157,12 @@ def tile_graphembedlayer_kernel(tc, pos, offs, out):
                 op=ALU.mult,
             )
 
-        def double(u, m, rows):
+        def double(u, m, rows, coords):
             low = HALF - 2 * m
             nc.vector.tensor_tensor(
-                out=upper[u][:, :, low : low + m, :],
-                in0=upper[u][:, :, low + m : low + 2 * m, :],
-                in1=factors[u][:, rows, :].unsqueeze(1).to_broadcast([SAMPLES, COORDS, m, BLOCK]),
+                out=upper[u][:, coords, low : low + m, :],
+                in0=upper[u][:, coords, low + m : low + 2 * m, :],
+                in1=factors[u][:, rows, :].unsqueeze(1).to_broadcast([SAMPLES, coords.stop - coords.start, m, BLOCK]),
                 op=ALU.mult,
             )
 
@@ -187,7 +189,7 @@ def tile_graphembedlayer_kernel(tc, pos, offs, out):
             for n in range(FULL):
                 sum_neighbours(bank[u, a][:, n : n + 1, :], lacking[:, n, :], lower[:, n : n + 1, :])
             staged = stage.tile([SAMPLES, BLOCK_ATOMS, RADIAL], F32, name="staged")
-            nc.any.tensor_copy(staged[:], bank[u, a][:].rearrange("p n i -> p i n"))
+            nc.scalar.copy(staged[:], bank[u, a][:].rearrange("p n i -> p i n"))
             nc.sync.dma_start(
                 out[a * SAMPLES : (a + 1) * SAMPLES, u * BANK : (u + 1) * BANK],
                 staged[:].rearrange("p i n -> p (i n)"),
@@ -203,10 +205,10 @@ def tile_graphembedlayer_kernel(tc, pos, offs, out):
                     if a == 0:
                         pivot_products(u)
                     elif a == 1:
-                        double(u, 1, slice(0, 1))
+                        double(u, 1, slice(0, 1), slice(0, COORDS))
                     else:
-                        double(u, 2, slice(1, 3))
                         for c in range(COORDS):
+                            double(u, 2, slice(1, 3), slice(c, c + 1))
                             begin(u, c)
                 if u > 0:
                     finish(u - 1, a)

@@ -30,9 +30,8 @@ SIGMA = 2.5 / RADIAL
 MU = [2.5 * n / (RADIAL - 1) for n in range(RADIAL)]
 PIVOT = RADIAL - 1
 DELTA = MU[1] - MU[0]
-FACTORS = ((1, 0), (2, 1), (2, 0), (4, 0))
-FULL = 3
-LACK = [math.exp(-4.0 * (FULL - n) * DELTA**2 / SIGMA**2) for n in range(FULL)]
+FACTORS = ((1, 0), (2, 1), (2, 0), (4, 2), (4, 0))
+LACK = math.exp(-4.0 * DELTA**2 / SIGMA**2)
 COL_PIVOT = len(FACTORS)
 COL_LOG_ANG = len(FACTORS) + 1
 
@@ -69,9 +68,8 @@ def tile_graphembedlayer_kernel(tc, pos, offs, out):
         make_identity(nc, identity_f32[:])
         identity_bf16 = held.tile([SAMPLES, SAMPLES], BF16, name="identity_bf16")
         make_identity(nc, identity_bf16[:])
-        lacking = held.tile([SAMPLES, FULL, SAMPLES], BF16, name="lacking")
-        for n in range(FULL):
-            nc.scalar.mul(lacking[:, n, :], identity_f32[:], LACK[n])
+        lacking = held.tile([SAMPLES, SAMPLES], BF16, name="lacking")
+        nc.scalar.mul(lacking[:], identity_f32[:], LACK)
 
         sine = [held.tile([SAMPLES, COORDS, PIECE], BF16, name=f"sine{k}") for k in range(PIECES)]
         q = []
@@ -178,16 +176,16 @@ def tile_graphembedlayer_kernel(tc, pos, offs, out):
             sum_neighbours(bank[u, a][:, HALF:RADIAL, :], identity_bf16[:], upper[u][:, a, :, :])
 
         def finish(u, a):
-            lower = lows.tile([SAMPLES, HALF, BLOCK], BF16, name="lower")
+            lower = lows.tile([SAMPLES, HALF // 2, 2, BLOCK], BF16, name="lower")
             nc.vector.tensor_tensor(
                 out=lower[:],
-                in0=upper[u][:, a, :, :],
-                in1=factors[u][:, 3:4, :].to_broadcast([SAMPLES, HALF, BLOCK]),
+                in0=upper[u][:, a, :, :].rearrange("p (g s) j -> p g s j", s=2),
+                in1=factors[u][:, 3:5, :].unsqueeze(2).to_broadcast([SAMPLES, HALF // 2, 2, BLOCK]),
                 op=ALU.mult,
             )
-            sum_neighbours(bank[u, a][:, FULL:HALF, :], identity_bf16[:], lower[:, FULL:HALF, :])
-            for n in range(FULL):
-                sum_neighbours(bank[u, a][:, n : n + 1, :], lacking[:, n, :], lower[:, n : n + 1, :])
+            pairs = bank[u, a][:, 0:HALF, :].rearrange("p (g s) i -> p g s i", s=2)
+            sum_neighbours(pairs[:, :, 1, :], identity_bf16[:], lower[:, :, 1, :])
+            sum_neighbours(pairs[:, :, 0, :], lacking[:], lower[:, :, 0, :])
             staged = stage.tile([SAMPLES, BLOCK_ATOMS, RADIAL], F32, name="staged")
             nc.scalar.copy(staged[:], bank[u, a][:].rearrange("p n i -> p i n"))
             nc.sync.dma_start(

@@ -31,6 +31,7 @@ MU = [2.5 * n / (RADIAL - 1) for n in range(RADIAL)]
 PIVOT = RADIAL - 1
 DELTA = MU[1] - MU[0]
 FACTORS = ((1, 0), (2, 1), (2, 0), (4, 2), (4, 0))
+ROWS = {1: slice(0, 1), 2: slice(1, 3), 4: slice(3, 5)}
 LACK = math.exp(-4.0 * DELTA**2 / SIGMA**2)
 COL_PIVOT = len(FACTORS)
 COL_LOG_ANG = len(FACTORS) + 1
@@ -42,9 +43,9 @@ def tile_graphembedlayer_kernel(tc, pos, offs, out):
         tc.tile_pool(name="held", bufs=1) as held,
         tc.tile_pool(name="ring", bufs=3) as ring,
         tc.tile_pool(name="ahead", bufs=AHEAD + 2) as ahead,
-        tc.tile_pool(name="lag", bufs=6) as lag,
-        tc.tile_pool(name="lows", bufs=6) as lows,
-        tc.tile_pool(name="stage", bufs=6) as stage,
+        tc.tile_pool(name="lag", bufs=2 * COORDS) as lag,
+        tc.tile_pool(name="lows", bufs=2 * COORDS) as lows,
+        tc.tile_pool(name="stage", bufs=2 * COORDS) as stage,
         tc.psum_pool(name="psum", bufs=BANKS) as psum,
     ):
         offsets = held.tile([SAMPLES, ATOMS * DEG // 16], U16, name="offsets")
@@ -155,12 +156,12 @@ def tile_graphembedlayer_kernel(tc, pos, offs, out):
                 op=ALU.mult,
             )
 
-        def double(u, m, rows, coords):
+        def double(u, m, coords):
             low = HALF - 2 * m
             nc.vector.tensor_tensor(
                 out=upper[u][:, coords, low : low + m, :],
                 in0=upper[u][:, coords, low + m : low + 2 * m, :],
-                in1=factors[u][:, rows, :].unsqueeze(1).to_broadcast([SAMPLES, coords.stop - coords.start, m, BLOCK]),
+                in1=factors[u][:, ROWS[m], :].unsqueeze(1).to_broadcast([SAMPLES, coords.stop - coords.start, m, BLOCK]),
                 op=ALU.mult,
             )
 
@@ -180,7 +181,7 @@ def tile_graphembedlayer_kernel(tc, pos, offs, out):
             nc.vector.tensor_tensor(
                 out=lower[:],
                 in0=upper[u][:, a, :, :].rearrange("p (g s) j -> p g s j", s=2),
-                in1=factors[u][:, 3:5, :].unsqueeze(2).to_broadcast([SAMPLES, HALF // 2, 2, BLOCK]),
+                in1=factors[u][:, ROWS[HALF], :].unsqueeze(2).to_broadcast([SAMPLES, HALF // 2, 2, BLOCK]),
                 op=ALU.mult,
             )
             pairs = bank[u, a][:, 0:HALF, :].rearrange("p (g s) i -> p g s i", s=2)
@@ -198,15 +199,16 @@ def tile_graphembedlayer_kernel(tc, pos, offs, out):
         for u in range(BLOCKS + 1):
             if u + AHEAD < BLOCKS:
                 exponentials(u + AHEAD)
-            for a in range(COORDS):
+            for step in range(COORDS):
                 if u < BLOCKS:
-                    if a == 0:
+                    if step == 0:
                         pivot_products(u)
-                    elif a == 1:
-                        double(u, 1, slice(0, 1), slice(0, COORDS))
+                    elif step == 1:
+                        double(u, 1, slice(0, COORDS))
                     else:
-                        for c in range(COORDS):
-                            double(u, 2, slice(1, 3), slice(c, c + 1))
-                            begin(u, c)
+                        for a in range(COORDS):
+                            double(u, 2, slice(a, a + 1))
+                        for a in range(COORDS):
+                            begin(u, a)
                 if u > 0:
-                    finish(u - 1, a)
+                    finish(u - 1, step)

@@ -93,6 +93,12 @@ def tile_graphembedlayer_kernel(tc, pos, offs, out):
 
         negate(COORDS - 1, nc.scalar.mul)
 
+        def square_on_scalar(k, a):
+            square = ring.tile([SAMPLES, PIECE], F32, name="square")
+            nc.scalar.activation(out=square[:], in_=sine[k][:, a, :], func=ACT.Square)
+            nc.tensor.matmul(q[k][:], identity_f32[:], square[:], start=(a == 0), stop=(a == COORDS - 1))
+
+        unsquared = None
         for k in range(PIECES):
             q.append(psum.tile([SAMPLES, PIECE], F32, name="q", tag="bank"))
             for a in range(COORDS):
@@ -111,10 +117,12 @@ def tile_graphembedlayer_kernel(tc, pos, offs, out):
                     func=ACT.Sin,
                     scale=1.0 / ANG,
                 )
-                if k < PIECES - 1:
-                    square = ring.tile([SAMPLES, PIECE], F32, name="square")
-                    nc.scalar.activation(out=square[:], in_=sine[k][:, a, :], func=ACT.Square)
-                    nc.tensor.matmul(q[k][:], identity_f32[:], square[:], start=(a == 0), stop=(a == COORDS - 1))
+                if k == 0 and a == 0:
+                    square_on_scalar(k, a)
+                else:
+                    if unsquared is not None:
+                        square_on_scalar(*unsquared)
+                    unsquared = (k, a) if k < PIECES - 1 else None
             if k == 1:
                 square_rho(0)
 

@@ -8,6 +8,7 @@ BF16 = mybir.dt.bfloat16
 U16 = mybir.dt.uint16
 ACT = mybir.ActivationFunctionType
 ALU = mybir.AluOpType
+AXIS = mybir.AxisListType
 
 SAMPLES = 128
 COORDS = 3
@@ -17,11 +18,14 @@ RADIAL = 8
 HALF = RADIAL // 2
 PIECE = 512
 PIECES = ATOMS * DEG // PIECE
+GROUP = 128
+GROUP_ATOMS = GROUP // DEG
+PIECE_GROUPS = PIECE // GROUP
 BANK = 512
-BANKS = 8
 BLOCK_ATOMS = BANK // RADIAL
-BLOCK = BLOCK_ATOMS * DEG
-PIECE_BLOCKS = PIECE // BLOCK
+BLOCK_GROUPS = BLOCK_ATOMS // GROUP_ATOMS
+BLOCK = BLOCK_GROUPS * SAMPLES
+PIECE_BLOCKS = PIECE_GROUPS // BLOCK_GROUPS
 BLOCKS = PIECES * PIECE_BLOCKS
 AHEAD = 2
 
@@ -30,11 +34,16 @@ SIGMA = 2.5 / RADIAL
 MU = [2.5 * n / (RADIAL - 1) for n in range(RADIAL)]
 PIVOT = RADIAL - 1
 DELTA = MU[1] - MU[0]
-FACTORS = ((1, 0), (2, 1), (2, 0), (4, 2), (4, 0))
-ROWS = {1: slice(0, 1), 2: slice(1, 3), 4: slice(3, 5)}
-LACK = math.exp(-4.0 * DELTA**2 / SIGMA**2)
-COL_PIVOT = len(FACTORS)
-COL_LOG_ANG = len(FACTORS) + 1
+STEPS = (1, 2, 4)
+ROW = {m: row for row, m in enumerate(STEPS)}
+COL_PIVOT = len(STEPS)
+COL_LOG_ANG = len(STEPS) + 1
+
+
+def lack(n):
+    taken = [m for m in STEPS if (PIVOT - n) & m]
+    pairs = sum(taken[i] * taken[j] for i in range(len(taken)) for j in range(i))
+    return math.exp(-pairs * DELTA**2 / SIGMA**2)
 
 
 def tile_graphembedlayer_kernel(tc, pos, offs, out):
@@ -46,7 +55,8 @@ def tile_graphembedlayer_kernel(tc, pos, offs, out):
         tc.tile_pool(name="lag", bufs=2 * COORDS) as lag,
         tc.tile_pool(name="lows", bufs=2 * COORDS) as lows,
         tc.tile_pool(name="stage", bufs=2 * COORDS) as stage,
-        tc.psum_pool(name="psum", bufs=BANKS) as psum,
+        tc.psum_pool(name="sums", bufs=1) as sums,
+        tc.psum_pool(name="work", bufs=4) as work,
     ):
         offsets = held.tile([SAMPLES, ATOMS * DEG // 16], U16, name="offsets")
         table = [held.tile([SAMPLES, ATOMS], F32, name=f"table{a}") for a in range(COORDS)]
@@ -56,10 +66,10 @@ def tile_graphembedlayer_kernel(tc, pos, offs, out):
         nc.sync.dma_start(table[2][:], pos[2 * SAMPLES : 3 * SAMPLES, :])
         nc.scalar.dma_start(table[1][:], pos[SAMPLES : 2 * SAMPLES, :])
 
-        biases = held.tile([SAMPLES, len(FACTORS) + 2], F32, name="biases")
-        for f, (m, d) in enumerate(FACTORS):
+        biases = held.tile([SAMPLES, len(STEPS) + 2], F32, name="biases")
+        for m in STEPS:
             nc.gpsimd.memset(
-                biases[:, f : f + 1], (m * DELTA * MU[PIVOT] - ((d + m) ** 2 - d**2) * DELTA**2 / 2) / SIGMA**2
+                biases[:, ROW[m] : ROW[m] + 1], (m * DELTA * MU[PIVOT] - (m * DELTA) ** 2 / 2) / SIGMA**2
             )
         nc.gpsimd.memset(biases[:, COL_PIVOT : COL_PIVOT + 1], -MU[PIVOT])
         nc.gpsimd.memset(biases[:, COL_LOG_ANG : COL_LOG_ANG + 1], math.log(ANG))
@@ -69,12 +79,17 @@ def tile_graphembedlayer_kernel(tc, pos, offs, out):
         make_identity(nc, identity_f32[:])
         identity_bf16 = held.tile([SAMPLES, SAMPLES], BF16, name="identity_bf16")
         make_identity(nc, identity_bf16[:])
-        lacking = held.tile([SAMPLES, SAMPLES], BF16, name="lacking")
-        nc.scalar.mul(lacking[:], identity_f32[:], LACK)
+        ones = held.tile([GROUP, GROUP_ATOMS], F32, name="ones")
+        nc.vector.tensor_reduce(
+            out=ones[:], in_=identity_f32[:].rearrange("p (i t) -> p i t", t=DEG), op=ALU.add, axis=AXIS.X
+        )
+        weigh = held.tile([GROUP, RADIAL, GROUP_ATOMS], BF16, name="weigh")
+        for n in range(RADIAL):
+            nc.vector.tensor_scalar_mul(weigh[:, n, :], ones[:], lack(n))
 
-        sine = [held.tile([SAMPLES, COORDS, PIECE], BF16, name=f"sine{k}") for k in range(PIECES)]
-        q = []
-        rho_sq = [held.tile([SAMPLES, PIECE], F32, name=f"rho_sq{k}") for k in range(PIECES)]
+        sine = [held.tile([GROUP, COORDS, PIECE], BF16, name=f"sine{k}") for k in range(PIECES)]
+        q = [sums.tile([GROUP, PIECE], F32, name=f"q{k}") for k in range(PIECES)]
+        rho_sq = [held.tile([GROUP, PIECE], F32, name=f"rho_sq{k}") for k in range(PIECES)]
 
         def square_rho(k):
             nc.scalar.activation(
@@ -82,121 +97,115 @@ def tile_graphembedlayer_kernel(tc, pos, offs, out):
                 scale=ANG**2, bias=biases[:, COL_PIVOT : COL_PIVOT + 1],
             )
 
-        negated = [held.tile([SAMPLES, ATOMS * DEG], F32, name=f"negated{a}") for a in range(COORDS)]
+        negated = {}
 
-        def negate(a, multiply):
+        def negate(k, a, multiply):
+            centres = slice(k * PIECE // DEG, (k + 1) * PIECE // DEG)
+            negated[k, a] = held.tile([SAMPLES, PIECE], F32, name=f"negated{k}_{a}")
             multiply(
-                negated[a][:].rearrange("p (i t) -> p i t", t=DEG),
-                table[a][:].unsqueeze(2).to_broadcast([SAMPLES, ATOMS, DEG]),
+                negated[k, a][:].rearrange("p (i t) -> p i t", t=DEG),
+                table[a][:, centres].unsqueeze(2).to_broadcast([SAMPLES, PIECE // DEG, DEG]),
                 -1.0,
             )
 
-        negate(COORDS - 1, nc.scalar.mul)
+        def add_to_q(k, a, square):
+            nc.tensor.matmul(q[k][:], identity_bf16[:], square, start=(a == 0), stop=(a == COORDS - 1))
 
-        def square_on_scalar(k, a):
-            square = ring.tile([SAMPLES, PIECE], F32, name="square")
-            nc.scalar.activation(out=square[:], in_=sine[k][:, a, :], func=ACT.Square)
-            nc.tensor.matmul(q[k][:], identity_f32[:], square[:], start=(a == 0), stop=(a == COORDS - 1))
-
-        unsquared = None
+        negate(0, COORDS - 1, nc.scalar.mul)
         for k in range(PIECES):
-            q.append(psum.tile([SAMPLES, PIECE], F32, name="q", tag="bank"))
             for a in range(COORDS):
-                if k == 0 and a < COORDS - 1:
-                    negate(a, nc.vector.tensor_scalar_mul)
+                if (k, a) not in negated:
+                    negate(k, a, nc.vector.tensor_scalar_mul)
                 diff = lag.tile([SAMPLES, PIECE], F32, name="diff")
                 nc.vector.tensor_tensor(
                     out=diff[:],
                     in0=table[a][:].indirect(offsets[:, k * PIECE // 16 : (k + 1) * PIECE // 16]),
-                    in1=negated[a][:, k * PIECE : (k + 1) * PIECE],
+                    in1=negated[k, a][:],
                     op=ALU.add,
                 )
+                turned = work.tile([GROUP, PIECE_GROUPS, SAMPLES], F32, name="turned", tag="work")
+                for g in range(PIECE_GROUPS):
+                    nc.tensor.transpose(turned[:, g, :], diff[:, g * GROUP : (g + 1) * GROUP], identity_f32[:])
                 nc.scalar.activation(
-                    out=sine[k][:, a, :].rearrange("p (h t i) -> p h i t", t=DEG, i=BLOCK_ATOMS),
-                    in_=diff[:].rearrange("p (h i t) -> p h i t", t=DEG, i=BLOCK_ATOMS),
-                    func=ACT.Sin,
-                    scale=1.0 / ANG,
+                    out=sine[k][:, a, :], in_=turned[:].rearrange("p g b -> p (g b)"), func=ACT.Sin, scale=1.0 / ANG
                 )
-                if k == 0 and a == 0:
-                    square_on_scalar(k, a)
-                else:
-                    if unsquared is not None:
-                        square_on_scalar(*unsquared)
-                    unsquared = (k, a) if k < PIECES - 1 else None
+                if k < PIECES // 2:
+                    square = ring.tile([GROUP, PIECE], BF16, name="square")
+                    nc.scalar.activation(out=square[:], in_=sine[k][:, a, :], func=ACT.Square)
+                    add_to_q(k, a, square[:])
+                if k + 1 < PIECES and a > 0:
+                    negate(k + 1, a, nc.scalar.mul)
             if k == 1:
                 square_rho(0)
 
-        for a in range(COORDS):
-            square = ring.tile([SAMPLES, PIECE], F32, name="square")
-            nc.vector.tensor_tensor(
-                out=square[:], in0=sine[PIECES - 1][:, a, :], in1=sine[PIECES - 1][:, a, :], op=ALU.mult
-            )
-            nc.tensor.matmul(
-                q[PIECES - 1][:], identity_f32[:], square[:], start=(a == 0), stop=(a == COORDS - 1)
-            )
+        for k in range(PIECES // 2, PIECES):
+            squares = ring.tile([GROUP, COORDS, PIECE], BF16, name="squares")
+            nc.vector.tensor_tensor(out=squares[:], in0=sine[k][:], in1=sine[k][:], op=ALU.mult)
+            for a in range(COORDS):
+                add_to_q(k, a, squares[:, a, :])
 
-        envelope, factors, upper, bank = {}, {}, {}, {}
+        envelope, factors, upper = {}, {}, {}
 
         def exponentials(u):
             k, h = divmod(u, PIECE_BLOCKS)
-            entries = slice(h * BLOCK, (h + 1) * BLOCK)
+            columns = slice(h * BLOCK, (h + 1) * BLOCK)
             if k > 0 and h == 0:
                 square_rho(k)
-            envelope[u] = ahead.tile([SAMPLES, BLOCK], BF16, name="envelope")
+            envelope[u] = ahead.tile([GROUP, BLOCK], BF16, name="envelope")
             nc.scalar.activation(
-                out=envelope[u][:], in_=rho_sq[k][:, entries], func=ACT.Exp,
+                out=envelope[u][:], in_=rho_sq[k][:, columns], func=ACT.Exp,
                 scale=-1.0 / (2.0 * SIGMA**2), bias=biases[:, COL_LOG_ANG : COL_LOG_ANG + 1],
             )
-            factors[u] = ahead.tile([SAMPLES, len(FACTORS), BLOCK], BF16, name="factors")
-            for f, (m, d) in enumerate(FACTORS):
+            factors[u] = ahead.tile([GROUP, len(STEPS), BLOCK], BF16, name="factors")
+            for m in STEPS:
                 nc.scalar.activation(
-                    out=factors[u][:, f, :], in_=q[k][:, entries], func=ACT.Exp,
-                    scale=-m * DELTA * ANG**2 / SIGMA**2, bias=biases[:, f : f + 1],
+                    out=factors[u][:, ROW[m], :], in_=q[k][:, columns], func=ACT.Exp,
+                    scale=-m * DELTA * ANG**2 / SIGMA**2, bias=biases[:, ROW[m] : ROW[m] + 1],
                 )
 
         def pivot_products(u):
             k, h = divmod(u, PIECE_BLOCKS)
-            upper[u] = ring.tile([SAMPLES, COORDS, HALF, BLOCK], BF16, name="upper")
+            upper[u] = ring.tile([GROUP, COORDS, HALF, BLOCK], BF16, name="upper")
             nc.vector.tensor_tensor(
                 out=upper[u][:, :, PIVOT - HALF, :],
                 in0=sine[k][:, :, h * BLOCK : (h + 1) * BLOCK],
-                in1=envelope[u][:].unsqueeze(1).to_broadcast([SAMPLES, COORDS, BLOCK]),
+                in1=envelope[u][:].unsqueeze(1).to_broadcast([GROUP, COORDS, BLOCK]),
                 op=ALU.mult,
             )
 
-        def double(u, m, coords):
+        def double(u, m):
             low = HALF - 2 * m
             nc.vector.tensor_tensor(
-                out=upper[u][:, coords, low : low + m, :],
-                in0=upper[u][:, coords, low + m : low + 2 * m, :],
-                in1=factors[u][:, ROWS[m], :].unsqueeze(1).to_broadcast([SAMPLES, coords.stop - coords.start, m, BLOCK]),
+                out=upper[u][:, :, low : low + m, :],
+                in0=upper[u][:, :, low + m : low + 2 * m, :],
+                in1=factors[u][:, ROW[m], :].unsqueeze(1).unsqueeze(1).to_broadcast([GROUP, COORDS, m, BLOCK]),
                 op=ALU.mult,
             )
 
-        def sum_neighbours(columns, weight, products):
-            for t in range(DEG):
+        def sum_neighbours(bank, n, products):
+            for g in range(BLOCK_GROUPS):
                 nc.tensor.matmul(
-                    columns, weight, products[:, :, t * BLOCK_ATOMS : (t + 1) * BLOCK_ATOMS],
-                    start=(t == 0), stop=(t == DEG - 1),
+                    bank[:, n, g * GROUP_ATOMS : (g + 1) * GROUP_ATOMS],
+                    products[:, g * SAMPLES : (g + 1) * SAMPLES],
+                    weigh[:, n, :],
+                    start=True, stop=True,
                 )
 
-        def begin(u, a):
-            bank[u, a] = psum.tile([SAMPLES, RADIAL, BLOCK_ATOMS], F32, name="bank", tag="bank")
-            sum_neighbours(bank[u, a][:, HALF:RADIAL, :], identity_bf16[:], upper[u][:, a, :, :])
-
         def finish(u, a):
-            lower = lows.tile([SAMPLES, HALF // 2, 2, BLOCK], BF16, name="lower")
+            bank = work.tile([SAMPLES, RADIAL, BLOCK_ATOMS], F32, name="bank", tag="work")
+            for n in range(HALF, RADIAL):
+                sum_neighbours(bank, n, upper[u][:, a, n - HALF, :])
+            lower = lows.tile([GROUP, HALF, BLOCK], BF16, name="lower")
             nc.vector.tensor_tensor(
                 out=lower[:],
-                in0=upper[u][:, a, :, :].rearrange("p (g s) j -> p g s j", s=2),
-                in1=factors[u][:, ROWS[HALF], :].unsqueeze(2).to_broadcast([SAMPLES, HALF // 2, 2, BLOCK]),
+                in0=upper[u][:, a, :, :],
+                in1=factors[u][:, ROW[HALF], :].unsqueeze(1).to_broadcast([GROUP, HALF, BLOCK]),
                 op=ALU.mult,
             )
-            pairs = bank[u, a][:, 0:HALF, :].rearrange("p (g s) i -> p g s i", s=2)
-            sum_neighbours(pairs[:, :, 1, :], identity_bf16[:], lower[:, :, 1, :])
-            sum_neighbours(pairs[:, :, 0, :], lacking[:], lower[:, :, 0, :])
+            for n in range(HALF):
+                sum_neighbours(bank, n, lower[:, n, :])
             staged = stage.tile([SAMPLES, BLOCK_ATOMS, RADIAL], F32, name="staged")
-            nc.scalar.copy(staged[:], bank[u, a][:].rearrange("p n i -> p i n"))
+            nc.scalar.copy(staged[:], bank[:].rearrange("p n i -> p i n"))
             nc.sync.dma_start(
                 out[a * SAMPLES : (a + 1) * SAMPLES, u * BANK : (u + 1) * BANK],
                 staged[:].rearrange("p i n -> p (i n)"),
@@ -211,12 +220,7 @@ def tile_graphembedlayer_kernel(tc, pos, offs, out):
                 if u < BLOCKS:
                     if step == 0:
                         pivot_products(u)
-                    elif step == 1:
-                        double(u, 1, slice(0, COORDS))
                     else:
-                        for a in range(COORDS):
-                            double(u, 2, slice(a, a + 1))
-                        for a in range(COORDS):
-                            begin(u, a)
+                        double(u, step)
                 if u > 0:
                     finish(u - 1, step)

@@ -22,6 +22,7 @@ GROUP = 128
 GROUP_ATOMS = GROUP // DEG
 PIECE_GROUPS = PIECE // GROUP
 BANK = 512
+BANKS = 8
 BLOCK_ATOMS = BANK // RADIAL
 BLOCK_GROUPS = BLOCK_ATOMS // GROUP_ATOMS
 BLOCK = BLOCK_GROUPS * SAMPLES
@@ -36,6 +37,7 @@ PIVOT = RADIAL - 1
 DELTA = MU[1] - MU[0]
 STEPS = (1, 2, 4)
 ROW = {m: row for row, m in enumerate(STEPS)}
+ENVELOPE = len(STEPS)
 COL_PIVOT = len(STEPS)
 COL_LOG_ANG = len(STEPS) + 1
 
@@ -55,14 +57,13 @@ def tile_graphembedlayer_kernel(tc, pos, offs, out):
         tc.tile_pool(name="lag", bufs=2 * COORDS) as lag,
         tc.tile_pool(name="lows", bufs=2 * COORDS) as lows,
         tc.tile_pool(name="stage", bufs=2 * COORDS) as stage,
-        tc.psum_pool(name="sums", bufs=1) as sums,
-        tc.psum_pool(name="work", bufs=4) as work,
+        tc.psum_pool(name="psum", bufs=BANKS) as psum,
     ):
         offsets = held.tile([SAMPLES, ATOMS * DEG // 16], U16, name="offsets")
         table = [held.tile([SAMPLES, ATOMS], F32, name=f"table{a}") for a in range(COORDS)]
+        nc.sync.dma_start(offsets[:], offs)
         nc.sync.dma_start(table[0][0 : SAMPLES // 2, :], pos[0 : SAMPLES // 2, :])
         nc.scalar.dma_start(table[0][SAMPLES // 2 : SAMPLES, :], pos[SAMPLES // 2 : SAMPLES, :])
-        nc.sync.dma_start(offsets[:], offs)
         nc.sync.dma_start(table[2][:], pos[2 * SAMPLES : 3 * SAMPLES, :])
         nc.scalar.dma_start(table[1][:], pos[SAMPLES : 2 * SAMPLES, :])
 
@@ -88,7 +89,7 @@ def tile_graphembedlayer_kernel(tc, pos, offs, out):
             nc.vector.tensor_scalar_mul(weigh[:, n, :], ones[:], lack(n))
 
         sine = [held.tile([GROUP, COORDS, PIECE], BF16, name=f"sine{k}") for k in range(PIECES)]
-        q = [sums.tile([GROUP, PIECE], F32, name=f"q{k}") for k in range(PIECES)]
+        q = []
         rho_sq = [held.tile([GROUP, PIECE], F32, name=f"rho_sq{k}") for k in range(PIECES)]
 
         def square_rho(k):
@@ -97,70 +98,76 @@ def tile_graphembedlayer_kernel(tc, pos, offs, out):
                 scale=ANG**2, bias=biases[:, COL_PIVOT : COL_PIVOT + 1],
             )
 
-        negated = {}
+        negated = [held.tile([SAMPLES, ATOMS * DEG], F32, name=f"negated{a}") for a in range(COORDS)]
 
-        def negate(k, a, multiply):
-            centres = slice(k * PIECE // DEG, (k + 1) * PIECE // DEG)
-            negated[k, a] = held.tile([SAMPLES, PIECE], F32, name=f"negated{k}_{a}")
+        def negate(a, pieces, multiply):
+            first, end = pieces.start * PIECE, pieces.stop * PIECE
             multiply(
-                negated[k, a][:].rearrange("p (i t) -> p i t", t=DEG),
-                table[a][:, centres].unsqueeze(2).to_broadcast([SAMPLES, PIECE // DEG, DEG]),
+                negated[a][:, first:end].rearrange("p (i t) -> p i t", t=DEG),
+                table[a][:, first // DEG : end // DEG].unsqueeze(2).to_broadcast([SAMPLES, (end - first) // DEG, DEG]),
                 -1.0,
             )
 
         def add_to_q(k, a, square):
             nc.tensor.matmul(q[k][:], identity_bf16[:], square, start=(a == 0), stop=(a == COORDS - 1))
 
-        negate(0, COORDS - 1, nc.scalar.mul)
+        negate(COORDS - 1, slice(0, 1), nc.scalar.mul)
+        for a in range(COORDS):
+            negate(a, slice(1, PIECES), nc.scalar.mul)
         for k in range(PIECES):
+            q.append(psum.tile([GROUP, PIECE], F32, name="q", tag="bank"))
             for a in range(COORDS):
-                if (k, a) not in negated:
-                    negate(k, a, nc.vector.tensor_scalar_mul)
+                if k == 0 and a < COORDS - 1:
+                    negate(a, slice(0, 1), nc.vector.tensor_scalar_mul)
                 diff = lag.tile([SAMPLES, PIECE], F32, name="diff")
                 nc.vector.tensor_tensor(
                     out=diff[:],
                     in0=table[a][:].indirect(offsets[:, k * PIECE // 16 : (k + 1) * PIECE // 16]),
-                    in1=negated[k, a][:],
+                    in1=negated[a][:, k * PIECE : (k + 1) * PIECE],
                     op=ALU.add,
                 )
-                turned = work.tile([GROUP, PIECE_GROUPS, SAMPLES], F32, name="turned", tag="work")
+                turned = psum.tile([GROUP, PIECE_GROUPS, SAMPLES], F32, name="turned", tag="bank")
                 for g in range(PIECE_GROUPS):
                     nc.tensor.transpose(turned[:, g, :], diff[:, g * GROUP : (g + 1) * GROUP], identity_f32[:])
                 nc.scalar.activation(
                     out=sine[k][:, a, :], in_=turned[:].rearrange("p g b -> p (g b)"), func=ACT.Sin, scale=1.0 / ANG
                 )
-                if k < PIECES // 2:
+                if k == 0:
                     square = ring.tile([GROUP, PIECE], BF16, name="square")
                     nc.scalar.activation(out=square[:], in_=sine[k][:, a, :], func=ACT.Square)
                     add_to_q(k, a, square[:])
-                if k + 1 < PIECES and a > 0:
-                    negate(k + 1, a, nc.scalar.mul)
             if k == 1:
                 square_rho(0)
 
-        for k in range(PIECES // 2, PIECES):
+        for k in range(1, PIECES):
             squares = ring.tile([GROUP, COORDS, PIECE], BF16, name="squares")
             nc.vector.tensor_tensor(out=squares[:], in0=sine[k][:], in1=sine[k][:], op=ALU.mult)
             for a in range(COORDS):
                 add_to_q(k, a, squares[:, a, :])
 
-        envelope, factors, upper = {}, {}, {}
+        exps, exps_psum, upper = {}, {}, {}
 
         def exponentials(u):
             k, h = divmod(u, PIECE_BLOCKS)
             columns = slice(h * BLOCK, (h + 1) * BLOCK)
             if k > 0 and h == 0:
                 square_rho(k)
-            envelope[u] = ahead.tile([GROUP, BLOCK], BF16, name="envelope")
+            exps[u] = ahead.tile([GROUP, len(STEPS) + 1, BLOCK], BF16, name="exps")
             nc.scalar.activation(
-                out=envelope[u][:], in_=rho_sq[k][:, columns], func=ACT.Exp,
+                out=exps[u][:, ENVELOPE, :], in_=rho_sq[k][:, columns], func=ACT.Exp,
                 scale=-1.0 / (2.0 * SIGMA**2), bias=biases[:, COL_LOG_ANG : COL_LOG_ANG + 1],
             )
-            factors[u] = ahead.tile([GROUP, len(STEPS), BLOCK], BF16, name="factors")
             for m in STEPS:
                 nc.scalar.activation(
-                    out=factors[u][:, ROW[m], :], in_=q[k][:, columns], func=ACT.Exp,
+                    out=exps[u][:, ROW[m], :], in_=q[k][:, columns], func=ACT.Exp,
                     scale=-m * DELTA * ANG**2 / SIGMA**2, bias=biases[:, ROW[m] : ROW[m] + 1],
+                )
+
+        def move_to_psum(u):
+            exps_psum[u] = psum.tile([GROUP, len(STEPS) + 1, BLOCK], BF16, name="exps_psum", tag="bank")
+            for rows in (slice(0, 2), slice(2, 4)):
+                nc.tensor.matmul(
+                    exps_psum[u][:, rows, :], identity_bf16[:], exps[u][:, rows, :], start=True, stop=True
                 )
 
         def pivot_products(u):
@@ -169,7 +176,7 @@ def tile_graphembedlayer_kernel(tc, pos, offs, out):
             nc.vector.tensor_tensor(
                 out=upper[u][:, :, PIVOT - HALF, :],
                 in0=sine[k][:, :, h * BLOCK : (h + 1) * BLOCK],
-                in1=envelope[u][:].unsqueeze(1).to_broadcast([GROUP, COORDS, BLOCK]),
+                in1=exps_psum[u][:, ENVELOPE, :].unsqueeze(1).to_broadcast([GROUP, COORDS, BLOCK]),
                 op=ALU.mult,
             )
 
@@ -178,7 +185,7 @@ def tile_graphembedlayer_kernel(tc, pos, offs, out):
             nc.vector.tensor_tensor(
                 out=upper[u][:, :, low : low + m, :],
                 in0=upper[u][:, :, low + m : low + 2 * m, :],
-                in1=factors[u][:, ROW[m], :].unsqueeze(1).unsqueeze(1).to_broadcast([GROUP, COORDS, m, BLOCK]),
+                in1=exps_psum[u][:, ROW[m], :].unsqueeze(1).unsqueeze(1).to_broadcast([GROUP, COORDS, m, BLOCK]),
                 op=ALU.mult,
             )
 
@@ -192,14 +199,15 @@ def tile_graphembedlayer_kernel(tc, pos, offs, out):
                 )
 
         def finish(u, a):
-            bank = work.tile([SAMPLES, RADIAL, BLOCK_ATOMS], F32, name="bank", tag="work")
+            bank = psum.tile([SAMPLES, RADIAL, BLOCK_ATOMS], F32, name="bank", tag="bank")
             for n in range(HALF, RADIAL):
                 sum_neighbours(bank, n, upper[u][:, a, n - HALF, :])
             lower = lows.tile([GROUP, HALF, BLOCK], BF16, name="lower")
-            nc.vector.tensor_tensor(
+            engine, source = (nc.vector, exps_psum[u]) if a < COORDS - 1 else (nc.gpsimd, exps[u])
+            engine.tensor_tensor(
                 out=lower[:],
                 in0=upper[u][:, a, :, :],
-                in1=factors[u][:, ROW[HALF], :].unsqueeze(1).to_broadcast([GROUP, HALF, BLOCK]),
+                in1=source[:, ROW[HALF], :].unsqueeze(1).to_broadcast([GROUP, HALF, BLOCK]),
                 op=ALU.mult,
             )
             for n in range(HALF):
@@ -213,9 +221,12 @@ def tile_graphembedlayer_kernel(tc, pos, offs, out):
 
         for u in range(AHEAD):
             exponentials(u)
+        move_to_psum(0)
         for u in range(BLOCKS + 1):
             if u + AHEAD < BLOCKS:
                 exponentials(u + AHEAD)
+            if u + 1 < BLOCKS:
+                move_to_psum(u + 1)
             for step in range(COORDS):
                 if u < BLOCKS:
                     if step == 0:

@@ -117,21 +117,26 @@ def tile_graphembedlayer_kernel(tc, pos, offs, out):
         for k in range(PIECES):
             q.append(psum.tile([GROUP, PIECE], F32, name="q", tag="bank"))
             for a in range(COORDS):
+                parts = 2 if (k, a) == (PIECES - 1, COORDS - 1) else 1
                 if k == 0 and a < COORDS - 1:
                     negate(a, slice(0, 1), nc.vector.tensor_scalar_mul)
-                diff = lag.tile([SAMPLES, PIECE], F32, name="diff")
-                nc.vector.tensor_tensor(
-                    out=diff[:],
-                    in0=table[a][:].indirect(offsets[:, k * PIECE // 16 : (k + 1) * PIECE // 16]),
-                    in1=negated[a][:, k * PIECE : (k + 1) * PIECE],
-                    op=ALU.add,
-                )
-                turned = psum.tile([GROUP, PIECE_GROUPS, SAMPLES], F32, name="turned", tag="bank")
-                for g in range(PIECE_GROUPS):
-                    nc.tensor.transpose(turned[:, g, :], diff[:, g * GROUP : (g + 1) * GROUP], identity_f32[:])
-                nc.scalar.activation(
-                    out=sine[k][:, a, :], in_=turned[:].rearrange("p g b -> p (g b)"), func=ACT.Sin, scale=1.0 / ANG
-                )
+                for part in range(parts):
+                    width = PIECE // parts
+                    first = k * PIECE + part * width
+                    diff = lag.tile([SAMPLES, width], F32, name="diff")
+                    nc.vector.tensor_tensor(
+                        out=diff[:],
+                        in0=table[a][:].indirect(offsets[:, first // 16 : (first + width) // 16]),
+                        in1=negated[a][:, first : first + width],
+                        op=ALU.add,
+                    )
+                    turned = psum.tile([GROUP, width], F32, name="turned", tag="bank")
+                    for group in range(0, width, GROUP):
+                        entries = slice(group, group + GROUP)
+                        nc.tensor.transpose(turned[:, entries], diff[:, entries], identity_f32[:])
+                    nc.scalar.activation(
+                        out=sine[k][:, a, part * width : (part + 1) * width], in_=turned[:], func=ACT.Sin, scale=1.0 / ANG
+                    )
                 if k == 0:
                     square = ring.tile([GROUP, PIECE], BF16, name="square")
                     nc.scalar.activation(out=square[:], in_=sine[k][:, a, :], func=ACT.Square)
@@ -170,13 +175,16 @@ def tile_graphembedlayer_kernel(tc, pos, offs, out):
                     exps_psum[u][:, rows, :], identity_bf16[:], exps[u][:, rows, :], start=True, stop=True
                 )
 
+        def upper_source(u):
+            return exps[u] if u == 0 else exps_psum[u]
+
         def pivot_products(u):
             k, h = divmod(u, PIECE_BLOCKS)
             upper[u] = ring.tile([GROUP, COORDS, HALF, BLOCK], BF16, name="upper")
             nc.vector.tensor_tensor(
                 out=upper[u][:, :, PIVOT - HALF, :],
                 in0=sine[k][:, :, h * BLOCK : (h + 1) * BLOCK],
-                in1=exps_psum[u][:, ENVELOPE, :].unsqueeze(1).to_broadcast([GROUP, COORDS, BLOCK]),
+                in1=upper_source(u)[:, ENVELOPE, :].unsqueeze(1).to_broadcast([GROUP, COORDS, BLOCK]),
                 op=ALU.mult,
             )
 
@@ -185,7 +193,7 @@ def tile_graphembedlayer_kernel(tc, pos, offs, out):
             nc.vector.tensor_tensor(
                 out=upper[u][:, :, low : low + m, :],
                 in0=upper[u][:, :, low + m : low + 2 * m, :],
-                in1=exps_psum[u][:, ROW[m], :].unsqueeze(1).unsqueeze(1).to_broadcast([GROUP, COORDS, m, BLOCK]),
+                in1=upper_source(u)[:, ROW[m], :].unsqueeze(1).unsqueeze(1).to_broadcast([GROUP, COORDS, m, BLOCK]),
                 op=ALU.mult,
             )
 
@@ -203,7 +211,8 @@ def tile_graphembedlayer_kernel(tc, pos, offs, out):
             for n in range(HALF, RADIAL):
                 sum_neighbours(bank, n, upper[u][:, a, n - HALF, :])
             lower = lows.tile([GROUP, HALF, BLOCK], BF16, name="lower")
-            engine, source = (nc.vector, exps_psum[u]) if a < COORDS - 1 else (nc.gpsimd, exps[u])
+            on_gpsimd = a == COORDS - 1 and u < BLOCKS - 1
+            engine, source = (nc.gpsimd, exps[u]) if on_gpsimd else (nc.vector, exps_psum[u])
             engine.tensor_tensor(
                 out=lower[:],
                 in0=upper[u][:, a, :, :],

@@ -8,7 +8,6 @@ BF16 = mybir.dt.bfloat16
 U16 = mybir.dt.uint16
 ACT = mybir.ActivationFunctionType
 ALU = mybir.AluOpType
-AXIS = mybir.AxisListType
 
 SAMPLES = 128
 COORDS = 3
@@ -53,17 +52,17 @@ def tile_graphembedlayer_kernel(tc, pos, offs, out):
     with (
         tc.tile_pool(name="held", bufs=1) as held,
         tc.tile_pool(name="ring", bufs=3) as ring,
-        tc.tile_pool(name="ahead", bufs=AHEAD + 2) as ahead,
+        tc.tile_pool(name="ahead", bufs=AHEAD + 4) as ahead,
         tc.tile_pool(name="lag", bufs=2 * COORDS) as lag,
         tc.tile_pool(name="lows", bufs=2 * COORDS) as lows,
-        tc.tile_pool(name="stage", bufs=2 * COORDS) as stage,
+        tc.tile_pool(name="stage", bufs=4 * COORDS) as stage,
         tc.psum_pool(name="psum", bufs=BANKS) as psum,
     ):
         offsets = held.tile([SAMPLES, ATOMS * DEG // 16], U16, name="offsets")
         table = [held.tile([SAMPLES, ATOMS], F32, name=f"table{a}") for a in range(COORDS)]
-        nc.sync.dma_start(offsets[:], offs)
         nc.sync.dma_start(table[0][0 : SAMPLES // 2, :], pos[0 : SAMPLES // 2, :])
         nc.scalar.dma_start(table[0][SAMPLES // 2 : SAMPLES, :], pos[SAMPLES // 2 : SAMPLES, :])
+        nc.sync.dma_start(offsets[:], offs)
         nc.sync.dma_start(table[2][:], pos[2 * SAMPLES : 3 * SAMPLES, :])
         nc.scalar.dma_start(table[1][:], pos[SAMPLES : 2 * SAMPLES, :])
 
@@ -74,21 +73,25 @@ def tile_graphembedlayer_kernel(tc, pos, offs, out):
             )
         nc.gpsimd.memset(biases[:, COL_PIVOT : COL_PIVOT + 1], -MU[PIVOT])
         nc.gpsimd.memset(biases[:, COL_LOG_ANG : COL_LOG_ANG + 1], math.log(ANG))
+        constants = held.tile([GROUP, RADIAL * GROUP_ATOMS], F32, name="constants")
+        for n in range(RADIAL):
+            nc.gpsimd.memset(constants[:, n * GROUP_ATOMS : (n + 1) * GROUP_ATOMS], lack(n))
+        for sign, base in ((1, 0), (-1, DEG - 1)):
+            nc.gpsimd.affine_select(
+                out=constants[:], in_=constants[:], compare_op=ALU.is_ge, fill=0.0,
+                base=base, channel_multiplier=sign, pattern=[[0, RADIAL], [-sign * DEG, GROUP_ATOMS]],
+            )
         warm = held.tile([SAMPLES, 1], F32, name="warm")
         nc.scalar.activation(out=warm[:], in_=biases[:, 0:1], func=ACT.Sin, scale=0.0)
         identity_f32 = held.tile([SAMPLES, SAMPLES], F32, name="identity_f32")
         make_identity(nc, identity_f32[:])
         identity_bf16 = held.tile([SAMPLES, SAMPLES], BF16, name="identity_bf16")
-        make_identity(nc, identity_bf16[:])
-        ones = held.tile([GROUP, GROUP_ATOMS], F32, name="ones")
-        nc.vector.tensor_reduce(
-            out=ones[:], in_=identity_f32[:].rearrange("p (i t) -> p i t", t=DEG), op=ALU.add, axis=AXIS.X
-        )
+        nc.scalar.copy(identity_bf16[:], identity_f32[:])
         weigh = held.tile([GROUP, RADIAL, GROUP_ATOMS], BF16, name="weigh")
-        for n in range(RADIAL):
-            nc.vector.tensor_scalar_mul(weigh[:, n, :], ones[:], lack(n))
+        nc.scalar.copy(weigh[:].rearrange("p n i -> p (n i)"), constants[:])
 
         sine = [held.tile([GROUP, COORDS, PIECE], BF16, name=f"sine{k}") for k in range(PIECES)]
+        squares = [held.tile([GROUP, COORDS, PIECE], BF16, name=f"squares{k}") for k in range(PIECES)]
         q = []
         rho_sq = [held.tile([GROUP, PIECE], F32, name=f"rho_sq{k}") for k in range(PIECES)]
 
@@ -97,6 +100,14 @@ def tile_graphembedlayer_kernel(tc, pos, offs, out):
                 out=rho_sq[k][:], in_=q[k][:], func=ACT.Square,
                 scale=ANG**2, bias=biases[:, COL_PIVOT : COL_PIVOT + 1],
             )
+
+        def transposed(tile, identity):
+            width = tile.shape[1]
+            turned = psum.tile([GROUP, width], tile.dtype, name="turned", tag="bank")
+            for group in range(0, width, GROUP):
+                entries = slice(group, group + GROUP)
+                nc.tensor.transpose(turned[:, entries], tile[:, entries], identity[:])
+            return turned
 
         negated = [held.tile([SAMPLES, ATOMS * DEG], F32, name=f"negated{a}") for a in range(COORDS)]
 
@@ -108,18 +119,21 @@ def tile_graphembedlayer_kernel(tc, pos, offs, out):
                 -1.0,
             )
 
-        def add_to_q(k, a, square):
-            nc.tensor.matmul(q[k][:], identity_bf16[:], square, start=(a == 0), stop=(a == COORDS - 1))
-
-        negate(COORDS - 1, slice(0, 1), nc.scalar.mul)
-        for a in range(COORDS):
-            negate(a, slice(1, PIECES), nc.scalar.mul)
-        for k in range(PIECES):
+        def sum_squares(k):
             q.append(psum.tile([GROUP, PIECE], F32, name="q", tag="bank"))
             for a in range(COORDS):
+                nc.tensor.matmul(
+                    q[k][:], identity_bf16[:], squares[k][:, a, :], start=(a == 0), stop=(a == COORDS - 1)
+                )
+
+        negate(0, slice(0, 1), nc.vector.tensor_scalar_mul)
+        for pieces in (slice(0, 1), slice(1, 2), slice(2, PIECES)):
+            for a in range(COORDS):
+                if pieces.start > 0 or a > 0:
+                    negate(a, pieces, nc.scalar.mul)
+        for k in range(PIECES):
+            for a in range(COORDS):
                 parts = 2 if (k, a) == (PIECES - 1, COORDS - 1) else 1
-                if k == 0 and a < COORDS - 1:
-                    negate(a, slice(0, 1), nc.vector.tensor_scalar_mul)
                 for part in range(parts):
                     width = PIECE // parts
                     first = k * PIECE + part * width
@@ -130,25 +144,24 @@ def tile_graphembedlayer_kernel(tc, pos, offs, out):
                         in1=negated[a][:, first : first + width],
                         op=ALU.add,
                     )
-                    turned = psum.tile([GROUP, width], F32, name="turned", tag="bank")
-                    for group in range(0, width, GROUP):
-                        entries = slice(group, group + GROUP)
-                        nc.tensor.transpose(turned[:, entries], diff[:, entries], identity_f32[:])
-                    nc.scalar.activation(
-                        out=sine[k][:, a, part * width : (part + 1) * width], in_=turned[:], func=ACT.Sin, scale=1.0 / ANG
-                    )
+                    columns = sine[k][:, a, part * width : (part + 1) * width]
+                    if k < PIECES - 1 or a == 0:
+                        nc.scalar.activation(
+                            out=columns, in_=transposed(diff, identity_f32)[:], func=ACT.Sin, scale=1.0 / ANG
+                        )
+                    else:
+                        early = ring.tile([SAMPLES, width], BF16, name="early")
+                        nc.scalar.activation(out=early[:], in_=diff[:], func=ACT.Sin, scale=1.0 / ANG)
+                        nc.vector.tensor_copy(columns, transposed(early, identity_bf16)[:])
                 if k == 0:
-                    square = ring.tile([GROUP, PIECE], BF16, name="square")
-                    nc.scalar.activation(out=square[:], in_=sine[k][:, a, :], func=ACT.Square)
-                    add_to_q(k, a, square[:])
+                    nc.scalar.activation(out=squares[k][:, a, :], in_=sine[k][:, a, :], func=ACT.Square)
             if k == 1:
+                sum_squares(0)
                 square_rho(0)
 
         for k in range(1, PIECES):
-            squares = ring.tile([GROUP, COORDS, PIECE], BF16, name="squares")
-            nc.vector.tensor_tensor(out=squares[:], in0=sine[k][:], in1=sine[k][:], op=ALU.mult)
-            for a in range(COORDS):
-                add_to_q(k, a, squares[:, a, :])
+            nc.vector.tensor_tensor(out=squares[k][:], in0=sine[k][:], in1=sine[k][:], op=ALU.mult)
+            sum_squares(k)
 
         exps, exps_psum, upper = {}, {}, {}
 
@@ -221,8 +234,9 @@ def tile_graphembedlayer_kernel(tc, pos, offs, out):
             )
             for n in range(HALF):
                 sum_neighbours(bank, n, lower[:, n, :])
+            copy = nc.vector.tensor_copy if (u, a) == (BLOCKS - 1, 1) else nc.scalar.copy
             staged = stage.tile([SAMPLES, BLOCK_ATOMS, RADIAL], F32, name="staged")
-            nc.scalar.copy(staged[:], bank[:].rearrange("p n i -> p i n"))
+            copy(staged[:], bank[:].rearrange("p n i -> p i n"))
             nc.sync.dma_start(
                 out[a * SAMPLES : (a + 1) * SAMPLES, u * BANK : (u + 1) * BANK],
                 staged[:].rearrange("p i n -> p (i n)"),

import math

import concourse.mybir as mybir
from concourse.masks import make_identity

F32 = mybir.dt.float32
BF16 = mybir.dt.bfloat16
U16 = mybir.dt.uint16
ACT = mybir.ActivationFunctionType
ALU = mybir.AluOpType

SAMPLES = 128
COORDS = 3
ATOMS = 512
DEG = 4
RADIAL = 8
HALF = RADIAL // 2
PIECE = 512
PIECES = ATOMS * DEG // PIECE
GROUP = 128
GROUP_ATOMS = GROUP // DEG
PIECE_GROUPS = PIECE // GROUP
BANK = 512
BANKS = 8
BLOCK_ATOMS = BANK // RADIAL
BLOCK_GROUPS = BLOCK_ATOMS // GROUP_ATOMS
BLOCK = BLOCK_GROUPS * SAMPLES
PIECE_BLOCKS = PIECE_GROUPS // BLOCK_GROUPS
BLOCKS = PIECES * PIECE_BLOCKS
AHEAD = 2

ANG = 6.0 / (2.0 * math.pi)
SIGMA = 2.5 / RADIAL
MU = [2.5 * n / (RADIAL - 1) for n in range(RADIAL)]
PIVOT = RADIAL - 1
DELTA = MU[1] - MU[0]
STEPS = (1, 2, 4)
ROW = {m: row for row, m in enumerate(STEPS)}
ENVELOPE = len(STEPS)
COL_PIVOT = len(STEPS)
COL_LOG_ANG = len(STEPS) + 1


def lack(n):
    taken = [m for m in STEPS if (PIVOT - n) & m]
    pairs = sum(taken[i] * taken[j] for i in range(len(taken)) for j in range(i))
    return math.exp(-pairs * DELTA**2 / SIGMA**2)


def tile_graphembedlayer_kernel(tc, pos, offs, out):
    nc = tc.nc
    with (
        tc.tile_pool(name="held", bufs=1) as held,
        tc.tile_pool(name="ring", bufs=3) as ring,
        tc.tile_pool(name="ahead", bufs=AHEAD + 4) as ahead,
        tc.tile_pool(name="lag", bufs=2 * COORDS) as lag,
        tc.tile_pool(name="lows", bufs=2 * COORDS) as lows,
        tc.tile_pool(name="stage", bufs=4 * COORDS) as stage,
        tc.psum_pool(name="psum", bufs=BANKS) as psum,
    ):
        offsets = held.tile([SAMPLES, ATOMS * DEG // 16], U16, name="offsets")
        table = [held.tile([SAMPLES, ATOMS], F32, name=f"table{a}") for a in range(COORDS)]
        nc.sync.dma_start(table[0][0 : SAMPLES // 2, :], pos[0 : SAMPLES // 2, :])
        nc.scalar.dma_start(table[0][SAMPLES // 2 : SAMPLES, :], pos[SAMPLES // 2 : SAMPLES, :])
        nc.sync.dma_start(offsets[:], offs)
        nc.sync.dma_start(table[2][:], pos[2 * SAMPLES : 3 * SAMPLES, :])
        nc.scalar.dma_start(table[1][:], pos[SAMPLES : 2 * SAMPLES, :])

        biases = held.tile([SAMPLES, len(STEPS) + 2], F32, name="biases")
        for m in STEPS:
            nc.gpsimd.memset(
                biases[:, ROW[m] : ROW[m] + 1], (m * DELTA * MU[PIVOT] - (m * DELTA) ** 2 / 2) / SIGMA**2
            )
        nc.gpsimd.memset(biases[:, COL_PIVOT : COL_PIVOT + 1], -MU[PIVOT])
        nc.gpsimd.memset(biases[:, COL_LOG_ANG : COL_LOG_ANG + 1], math.log(ANG))
        constants = held.tile([GROUP, RADIAL * GROUP_ATOMS], F32, name="constants")
        for n in range(RADIAL):
            nc.gpsimd.memset(constants[:, n * GROUP_ATOMS : (n + 1) * GROUP_ATOMS], lack(n))
        for sign, base in ((1, 0), (-1, DEG - 1)):
            nc.gpsimd.affine_select(
                out=constants[:], in_=constants[:], compare_op=ALU.is_ge, fill=0.0,
                base=base, channel_multiplier=sign, pattern=[[0, RADIAL], [-sign * DEG, GROUP_ATOMS]],
            )
        warm = held.tile([SAMPLES, 1], F32, name="warm")
        nc.scalar.activation(out=warm[:], in_=biases[:, 0:1], func=ACT.Sin, scale=0.0)
        identity_f32 = held.tile([SAMPLES, SAMPLES], F32, name="identity_f32")
        make_identity(nc, identity_f32[:])
        identity_bf16 = held.tile([SAMPLES, SAMPLES], BF16, name="identity_bf16")
        nc.scalar.copy(identity_bf16[:], identity_f32[:])
        weigh = held.tile([GROUP, RADIAL, GROUP_ATOMS], BF16, name="weigh")
        nc.scalar.copy(weigh[:].rearrange("p n i -> p (n i)"), constants[:])

        sine = [held.tile([GROUP, COORDS, PIECE], BF16, name=f"sine{k}") for k in range(PIECES)]
        squares = [held.tile([GROUP, COORDS, PIECE], BF16, name=f"squares{k}") for k in range(PIECES)]
        q = []
        rho_sq = [held.tile([GROUP, PIECE], F32, name=f"rho_sq{k}") for k in range(PIECES)]

        def square_rho(k):
            nc.scalar.activation(
                out=rho_sq[k][:], in_=q[k][:], func=ACT.Square,
                scale=ANG**2, bias=biases[:, COL_PIVOT : COL_PIVOT + 1],
            )

        def transposed(tile, identity):
            width = tile.shape[1]
            turned = psum.tile([GROUP, width], tile.dtype, name="turned", tag="bank")
            for group in range(0, width, GROUP):
                entries = slice(group, group + GROUP)
                nc.tensor.transpose(turned[:, entries], tile[:, entries], identity[:])
            return turned

        negated = [held.tile([SAMPLES, ATOMS * DEG], F32, name=f"negated{a}") for a in range(COORDS)]

        def negate(a, pieces, multiply):
            first, end = pieces.start * PIECE, pieces.stop * PIECE
            multiply(
                negated[a][:, first:end].rearrange("p (i t) -> p i t", t=DEG),
                table[a][:, first // DEG : end // DEG].unsqueeze(2).to_broadcast([SAMPLES, (end - first) // DEG, DEG]),
                -1.0,
            )

        def sum_squares(k):
            q.append(psum.tile([GROUP, PIECE], F32, name="q", tag="bank"))
            for a in range(COORDS):
                nc.tensor.matmul(
                    q[k][:], identity_bf16[:], squares[k][:, a, :], start=(a == 0), stop=(a == COORDS - 1)
                )

        negate(0, slice(0, 1), nc.vector.tensor_scalar_mul)
        for pieces in (slice(0, 1), slice(1, 2), slice(2, PIECES)):
            for a in range(COORDS):
                if pieces.start > 0 or a > 0:
                    negate(a, pieces, nc.scalar.mul)
        for k in range(PIECES):
            for a in range(COORDS):
                parts = 2 if (k, a) == (PIECES - 1, COORDS - 1) else 1
                for part in range(parts):
                    width = PIECE // parts
                    first = k * PIECE + part * width
                    diff = lag.tile([SAMPLES, width], F32, name="diff")
                    nc.vector.tensor_tensor(
                        out=diff[:],
                        in0=table[a][:].indirect(offsets[:, first // 16 : (first + width) // 16]),
                        in1=negated[a][:, first : first + width],
                        op=ALU.add,
                    )
                    columns = sine[k][:, a, part * width : (part + 1) * width]
                    if k < PIECES - 1 or a == 0:
                        nc.scalar.activation(
                            out=columns, in_=transposed(diff, identity_f32)[:], func=ACT.Sin, scale=1.0 / ANG
                        )
                    else:
                        early = ring.tile([SAMPLES, width], BF16, name="early")
                        nc.scalar.activation(out=early[:], in_=diff[:], func=ACT.Sin, scale=1.0 / ANG)
                        nc.vector.tensor_copy(columns, transposed(early, identity_bf16)[:])
                if k == 0:
                    nc.scalar.activation(out=squares[k][:, a, :], in_=sine[k][:, a, :], func=ACT.Square)
            if k == 1:
                sum_squares(0)
                square_rho(0)

        for k in range(1, PIECES):
            nc.vector.tensor_tensor(out=squares[k][:], in0=sine[k][:], in1=sine[k][:], op=ALU.mult)
            sum_squares(k)

        exps, exps_psum, upper = {}, {}, {}

        def exponentials(u):
            k, h = divmod(u, PIECE_BLOCKS)
            columns = slice(h * BLOCK, (h + 1) * BLOCK)
            if k > 0 and h == 0:
                square_rho(k)
            exps[u] = ahead.tile([GROUP, len(STEPS) + 1, BLOCK], BF16, name="exps")
            nc.scalar.activation(
                out=exps[u][:, ENVELOPE, :], in_=rho_sq[k][:, columns], func=ACT.Exp,
                scale=-1.0 / (2.0 * SIGMA**2), bias=biases[:, COL_LOG_ANG : COL_LOG_ANG + 1],
            )
            for m in STEPS:
                nc.scalar.activation(
                    out=exps[u][:, ROW[m], :], in_=q[k][:, columns], func=ACT.Exp,
                    scale=-m * DELTA * ANG**2 / SIGMA**2, bias=biases[:, ROW[m] : ROW[m] + 1],
                )

        def move_to_psum(u):
            exps_psum[u] = psum.tile([GROUP, len(STEPS) + 1, BLOCK], BF16, name="exps_psum", tag="bank")
            for rows in (slice(0, 2), slice(2, 4)):
                nc.tensor.matmul(
                    exps_psum[u][:, rows, :], identity_bf16[:], exps[u][:, rows, :], start=True, stop=True
                )

        def upper_source(u):
            return exps[u] if u == 0 else exps_psum[u]

        def pivot_products(u):
            k, h = divmod(u, PIECE_BLOCKS)
            upper[u] = ring.tile([GROUP, COORDS, HALF, BLOCK], BF16, name="upper")
            nc.vector.tensor_tensor(
                out=upper[u][:, :, PIVOT - HALF, :],
                in0=sine[k][:, :, h * BLOCK : (h + 1) * BLOCK],
                in1=upper_source(u)[:, ENVELOPE, :].unsqueeze(1).to_broadcast([GROUP, COORDS, BLOCK]),
                op=ALU.mult,
            )

        def double(u, m):
            low = HALF - 2 * m
            nc.vector.tensor_tensor(
                out=upper[u][:, :, low : low + m, :],
                in0=upper[u][:, :, low + m : low + 2 * m, :],
                in1=upper_source(u)[:, ROW[m], :].unsqueeze(1).unsqueeze(1).to_broadcast([GROUP, COORDS, m, BLOCK]),
                op=ALU.mult,
            )

        def sum_neighbours(bank, n, products):
            for g in range(BLOCK_GROUPS):
                nc.tensor.matmul(
                    bank[:, n, g * GROUP_ATOMS : (g + 1) * GROUP_ATOMS],
                    products[:, g * SAMPLES : (g + 1) * SAMPLES],
                    weigh[:, n, :],
                    start=True, stop=True,
                )

        def finish(u, a):
            bank = psum.tile([SAMPLES, RADIAL, BLOCK_ATOMS], F32, name="bank", tag="bank")
            for n in range(HALF, RADIAL):
                sum_neighbours(bank, n, upper[u][:, a, n - HALF, :])
            lower = lows.tile([GROUP, HALF, BLOCK], BF16, name="lower")
            on_gpsimd = a == COORDS - 1 and u < BLOCKS - 1
            engine, source = (nc.gpsimd, exps[u]) if on_gpsimd else (nc.vector, exps_psum[u])
            engine.tensor_tensor(
                out=lower[:],
                in0=upper[u][:, a, :, :],
                in1=source[:, ROW[HALF], :].unsqueeze(1).to_broadcast([GROUP, HALF, BLOCK]),
                op=ALU.mult,
            )
            for n in range(HALF):
                sum_neighbours(bank, n, lower[:, n, :])
            copy = nc.vector.tensor_copy if (u, a) == (BLOCKS - 1, 1) else nc.scalar.copy
            staged = stage.tile([SAMPLES, BLOCK_ATOMS, RADIAL], F32, name="staged")
            copy(staged[:], bank[:].rearrange("p n i -> p i n"))
            nc.sync.dma_start(
                out[a * SAMPLES : (a + 1) * SAMPLES, u * BANK : (u + 1) * BANK],
                staged[:].rearrange("p i n -> p (i n)"),
            )

        for u in range(AHEAD):
            exponentials(u)
        move_to_psum(0)
        for u in range(BLOCKS + 1):
            if u + AHEAD < BLOCKS:
                exponentials(u + AHEAD)
            if u + 1 < BLOCKS:
                move_to_psum(u + 1)
            for step in range(COORDS):
                if u < BLOCKS:
                    if step == 0:
                        pivot_products(u)
                    else:
                        double(u, step)
                if u > 0:
                    finish(u - 1, step)
